import numpy as np
import ml_dtypes


def mxq(x, axis, fmt="e4m3"):
    dtype, down = {"e4m3": (ml_dtypes.float8_e4m3fn, 7), "e5m2": (ml_dtypes.float8_e5m2, 14)}[fmt]
    v = np.moveaxis(np.asarray(x, np.float32).astype(ml_dtypes.bfloat16).astype(np.float64), axis, -1)
    blocks = v.reshape(v.shape[:-1] + (-1, 32))
    amax = np.abs(blocks).max(-1, keepdims=True)
    byte = np.maximum(np.where(amax > 0, np.frexp(amax)[1] - 1 + 127, 0) - down, 1)
    scale = np.exp2(byte - 127.0)
    codes = (blocks / scale).astype(np.float32).astype(dtype).astype(np.float64)
    return np.moveaxis((codes * scale).reshape(v.shape), -1, axis)


WIDE = False


def mx_kscale(k):
    if not WIDE:
        return np.ones(k)
    levels = np.array([10, -10, 5, -5, 0])
    if k % 512:
        return np.exp2(np.random.permutation(np.resize(levels, k // 32))).repeat(32)
    a = np.empty((k // 512, 16))
    for p in range(k // 512):
        a[p, :8] = np.random.permutation(np.resize(levels, 8))
        for g in range(8):
            far = levels[np.abs(levels - a[p, g]) >= 10]
            a[p, g + 8] = far[np.random.randint(len(far))]
    return np.exp2(a.ravel()).repeat(32)


BF16 = ml_dtypes.bfloat16


def bf(x):
    return np.asarray(x, np.float32).astype(BF16)


def f64(x):
    return np.asarray(x).astype(np.float64)


B, S, D, M, R = 128, 16, 2048, 8, 1024
LN_EPS = 1e-5


def sigmoid(v):
    return 1.0 / (1.0 + np.exp(-v))


def layer_norm(x):
    mu = np.mean(x, axis=-1, keepdims=True)
    var = np.var(x, axis=-1, keepdims=True)
    return (x - mu) / np.sqrt(var + LN_EPS)


def setup_inputs():
    s, t = mx_kscale(D), mx_kscale(R)
    return {"interface": bf(np.random.standard_normal((B, S, D)) * np.sqrt(S) * s),
            "memory": bf(0.5 + np.random.standard_normal((B, M, D))),
            "W_write_key": bf(np.random.standard_normal((R, D)) / np.sqrt(D) / s[None, :] * t[:, None]),
            "W_write_erase": bf(np.random.standard_normal((D, R)) * 1.5 / np.sqrt(R) / t[None, :]),
            "W_write_add": bf(np.random.standard_normal((D, R)) / np.sqrt(R) / t[None, :])}


def reference(interface, memory, W_write_key, W_write_erase, W_write_add):
    i_mean = np.mean(f64(interface), axis=1)
    i_proj = mxq(i_mean, 1, "e4m3") @ mxq(f64(W_write_key), 1, "e4m3").T
    pq = mxq(i_proj, 1, "e4m3")
    erase = sigmoid(pq @ mxq(f64(W_write_erase), 1, "e4m3").T)[:, None, :]
    add = (pq @ mxq(f64(W_write_add), 1, "e4m3").T)[:, None, :]
    return layer_norm(f64(memory) * (1.0 - erase) + add)

@@ -1,0 +1,450 @@
+from contextlib import ExitStack
+
+import concourse.masks as masks
+import concourse.mybir as mybir
+
+FLOPS = 2 * 128 * 2048 * 1024 * 3
+
+F32 = mybir.dt.float32
+BF16 = mybir.dt.bfloat16
+U32 = mybir.dt.uint32
+U8 = mybir.dt.uint8
+FP8X4 = mybir.dt.float8_e4m3fn_x4
+ALU = mybir.AluOpType
+ACT = mybir.ActivationFunctionType
+
+P = 128
+D = 2048
+ROWS = 4
+CHUNK = 512
+LN_EPS = 1e-5
+STEPS = 16
+LAST_PIECES = 4
+
+SLOT_OF = {
+    "k0": 0, "y00": 0,
+    "k1": 1, "y01": 1,
+    "x0": 2, "a0": 2, "y10": 2,
+    "x1": 3, "a1": 3, "y11": 3,
+    "e0": 4, "x2": 4,
+    "e1": 5, "x3": 5,
+}
+ADD_BANK = [2, 3, 4, 5]
+
+
+def tile_ultralightweightmemory_pa_kernel(
+    tc, interface, memory, W_write_key, W_write_erase, W_write_add, out
+):
+    nc = tc.nc
+    with ExitStack() as ctx:
+        const = ctx.enter_context(tc.tile_pool(name="const", bufs=1))
+        keep = ctx.enter_context(tc.tile_pool(name="keep", bufs=1))
+        slots = ctx.enter_context(tc.tile_pool(name="slots", bufs=1))
+        grouped = ctx.enter_context(tc.tile_pool(name="grouped", bufs=4))
+        psum = ctx.enter_context(tc.psum_pool(name="psum", bufs=1))
+        ctx.enter_context(tc.manual_schedule())
+
+        def bank(n, shape, dtype, name):
+            return psum.tile(shape, dtype, tag="bank%d" % n, name=name)
+
+        x_v = interface.rearrange("b s d -> (b s) d").rearrange("(T p i) d -> T p (i d)", p=P, i=2)
+        wk_v = W_write_key.rearrange("(G p h e) d -> G h p (e d)", p=P, h=2, e=2)
+        w2_v = {
+            "e": W_write_erase.rearrange("(I h p c) r -> I p h (c r)", h=2, p=P, c=2),
+            "a": W_write_add.rearrange("(I h p c) r -> I p h (c r)", h=2, p=P, c=2),
+        }
+        mem_v = memory.rearrange("b (u l) n -> (b u) (l n)", u=2)
+        out_v = out.rearrange("b (u l) n -> (b u) (l n)", u=2)
+
+        mem_sb = [keep.tile([P, ROWS * D], BF16, name="mem%d" % half) for half in range(2)]
+        gate_sb = keep.tile([P, D], F32)
+        squares = keep.tile([P, D], BF16)
+        words = {}
+        scales = {}
+        for kind in "kea":
+            words[kind] = keep.tile([P, 4096], U32, name="words_%s" % kind, align_bytes=64)
+            scales[kind] = keep.tile([P, 4096], U8, name="scales_%s" % kind, align_bytes=64)
+        mean_bf = keep.tile([P, 2048], BF16, align_bytes=64)
+        mean_words = keep.tile([P, 512], U32, align_bytes=64)
+        mean_scales = keep.tile([P, 512], U8, align_bytes=64)
+        proj_bf = keep.tile([P, 1024], BF16, align_bytes=64)
+        proj_words = keep.tile([P, 256], U32, align_bytes=64)
+        proj_scales = keep.tile([P, 256], U8, align_bytes=64)
+        part_sums = keep.tile([P, 2 * ROWS, 4], F32)
+        neg_sum = keep.tile([P, 2 * ROWS], F32)
+        neg_mean = keep.tile([P, 2 * ROWS], F32)
+        sq_sum = keep.tile([P, 2 * ROWS], F32)
+        var_eps = keep.tile([P, 2 * ROWS], F32)
+        rstd = keep.tile([P, 2 * ROWS], F32)
+        table_warm = keep.tile([P, 1], F32)
+
+        raw = {}
+        slot_tile = {}
+
+        def load(kind, idx):
+            if kind == "m":
+                half, part = divmod(idx, 2)
+                cols = slice(2 * D * part, 2 * D * (part + 1))
+                nc.sync.dma_start(out=mem_sb[half][:, cols], in_=mem_v[P * half : P * (half + 1), cols])
+                return
+            if idx % 2 == 0:
+                slot_tile[(kind, idx // 2)] = slots.tile(
+                    [P, 8192], BF16, tag="slot%d" % SLOT_OF["%s%d" % (kind, idx // 2)], name="raw_%s%d" % (kind, idx // 2)
+                )
+            t = slot_tile[(kind, idx // 2)][:, 4096 * (idx % 2) : 4096 * (idx % 2 + 1)]
+            if kind == "k":
+                nc.sync.dma_start(out=t, in_=wk_v[idx // 2, idx % 2])
+            elif kind == "x":
+                nc.sync.dma_start(out=t, in_=x_v[idx])
+            else:
+                nc.sync.dma_start(out=t.rearrange("p (h x) -> p h x", h=2), in_=w2_v[kind][idx])
+            raw[(kind, idx)] = t
+
+        for i in range(4):
+            load("k", i)
+        for i in range(4):
+            load("x", i)
+        for i in range(4):
+            load("e", i)
+
+        ident_f = const.tile([P, P], F32)
+        masks.make_identity(nc, ident_f[:])
+        ident_b = const.tile([P, P], BF16)
+        masks.make_identity(nc, ident_b[:])
+        member = const.tile([P, 16], F32)
+        nc.vector.tensor_reduce(
+            out=member[:], in_=ident_f[:].rearrange("p (n s) -> p n s", s=8), axis=mybir.AxisListType.X, op=ALU.add
+        )
+        averager = const.tile([P, 16], BF16)
+        nc.vector.tensor_scalar_mul(out=averager[:], in0=member[:], scalar1=1.0 / 16.0)
+        minus_half = const.tile([P, 1], F32)
+        nc.vector.memset(minus_half[:], -0.5)
+        nc.scalar.activation(out=table_warm[:], in_=minus_half[:], func=ACT.Sigmoid)
+
+        def copy_out(engine, dst, src):
+            if engine == "v":
+                nc.vector.tensor_copy(out=dst, in_=src)
+            else:
+                nc.scalar.copy(out=dst, in_=src)
+
+        def quantise(words_ap, scales_ap, in_ap):
+            nc.vector.quantize_mx(out=words_ap.bitcast(FP8X4), scales=scales_ap, in_=in_ap)
+
+        waiting = []
+
+        def quantise_waiting(keep_back):
+            while len(waiting) > keep_back:
+                waiting.pop(0)()
+
+        turn = {"n": 0}
+
+        def transpose_bank(shape, dtype, name, banks=4):
+            turn["n"] += 1
+            return bank(8 - banks + turn["n"] % banks, shape, dtype, name)
+
+        def prepare_key(j, e):
+            loaded = raw[("k", j)]
+            ce = 2 * j + e
+            group = grouped.tile([P, 2048], BF16, tag="grp", name="gk%d" % ce, align_bytes=64)
+            for g in range(4):
+                tp = transpose_bank([P, 4, P], BF16, "tpk%d_%d" % (ce, g))
+                for t in range(4):
+                    d0 = e * D + 512 * g
+                    nc.tensor.transpose(tp[:, t, :], loaded[:, d0 + t : d0 + 512 : 4], ident_b[:])
+                copy_out(
+                    "vs"[g % 2],
+                    group[:, 512 * g : 512 * (g + 1)].rearrange("p (c t) -> p c t", t=4),
+                    tp[:].rearrange("p t c -> p c t"),
+                )
+            cols = slice(512 * ce, 512 * (ce + 1))
+            waiting.append(lambda: quantise(words["k"][:, cols], scales["k"][:, cols], group[:]))
+            quantise_waiting(1)
+
+        mean_ps = {}
+
+        def mean_chunk(T):
+            half, Tl = divmod(T, 4)
+            if Tl == 0:
+                mean_ps[half] = [bank(z, [P, 8, 64], F32, "mean%d_%d" % (half, z)) for z in range(2)]
+            xt = raw[("x", T)]
+            for c in range(16):
+                for i in range(2):
+                    lo = i * D + 512 * (c // 4)
+                    nc.tensor.matmul(
+                        mean_ps[half][c // 8][:, c % 8, 16 * Tl : 16 * (Tl + 1)],
+                        lhsT=xt[:, lo + c % 4 : lo + 512 : 4],
+                        rhs=averager[:],
+                        start=(i == 0),
+                        stop=(i == 1),
+                    )
+
+        def mean_out(half):
+            for z in range(2):
+                for g in (z, 2 + z):
+                    src = mean_ps[half][g // 2][:, 4 * (g % 2) : 4 * (g % 2) + 4, :]
+                    copy_out(
+                        "vs"[g // 2],
+                        mean_bf[:, 512 * g : 512 * (g + 1)].rearrange("p (b u t) -> p b u t", u=2, t=4),
+                        src.rearrange("p t b -> p b t").unsqueeze(2).to_broadcast([P, 64, 2, 4]),
+                    )
+            quantise(mean_words[:, 0:256], mean_scales[:, 0:256], mean_bf[:, 0:1024])
+            quantise(mean_words[:, 256:512], mean_scales[:, 256:512], mean_bf[:, 1024:2048])
+
+        proj_ps = {}
+
+        def first_matmul(half, G):
+            pj = bank(2 + 4 * half + G, [P, 4, P], F32, "pj%d_%d" % (half, G))
+            proj_ps[G] = pj
+            for t in range(4):
+                ce = 4 * G + t
+                for g in range(4):
+                    lo = 512 * ce + 128 * g
+                    nc.tensor.matmul_mx(
+                        out=pj[:, t, :],
+                        lhsT=words["k"][:, lo : lo + 128].bitcast(FP8X4),
+                        lhsT_scale=scales["k"][:, lo : lo + 128],
+                        rhs=mean_words[:, 128 * g : 128 * (g + 1)].bitcast(FP8X4),
+                        rhs_scale=mean_scales[:, 128 * g : 128 * (g + 1)],
+                        start=(g == 0),
+                        stop=(g == 3),
+                    )
+
+        def proj_out(G):
+            copy_out(
+                "v",
+                proj_bf[:, 512 * G : 512 * (G + 1)].rearrange("p (b t) -> p b t", t=4),
+                proj_ps[G][:].rearrange("p t b -> p b t"),
+            )
+            cols = slice(128 * G, 128 * (G + 1))
+            quantise(proj_words[:, cols], proj_scales[:, cols], proj_bf[:, 512 * G : 512 * (G + 1)])
+
+        chunks = [("e", I) for I in range(4)] + [("a", I) for I in range(4)]
+
+        def prepare(step):
+            kind, I = chunks[step // 2]
+            h = step % 2
+            r_pairs = raw[(kind, I)].bitcast(F32)
+            group = grouped.tile([P, 2048], BF16, tag="grp", name="gw%d" % step, align_bytes=64)
+            group_r_pairs = group[:].bitcast(F32)
+            for G in range(2):
+                tp = transpose_bank([P, 2, 2, P], F32, "tpw%d_%d" % (step, G), 2 if step >= STEPS - 2 else 4)
+                for c in range(2):
+                    for u in range(2):
+                        w0 = (h * 2 + c) * 512 + 256 * G
+                        nc.tensor.transpose(tp[:, c, u, :], r_pairs[:, w0 + u : w0 + 256 : 2], ident_f[:])
+                copy_out(
+                    "s",
+                    group_r_pairs[:, 512 * G : 512 * (G + 1)].rearrange("q (p c u) -> q p c u", c=2, u=2),
+                    tp[:].rearrange("q c u p -> q p c u"),
+                )
+            if kind == "e" and step % 4 == 3:
+                load("x", 3 + I)
+                load("x", 4 + I)
+                if I == 3:
+                    load("m", 2)
+                    load("m", 3)
+            cols = slice(512 * (2 * I + h), 512 * (2 * I + h + 1))
+            waiting.append(lambda: quantise(words[kind][:, cols], scales[kind][:, cols], group[:]))
+
+        def second_matmul(o_ps, kind, I):
+            for h in range(2):
+                for G in range(2):
+                    lo = 512 * (2 * I + h) + 256 * G
+                    nc.tensor.matmul_mx(
+                        out=o_ps[:, 256 * h : 256 * (h + 1)],
+                        lhsT=proj_words[:, 128 * G : 128 * (G + 1)].bitcast(FP8X4),
+                        lhsT_scale=proj_scales[:, 128 * G : 128 * (G + 1)],
+                        rhs=words[kind][:, lo : lo + 256].bitcast(FP8X4),
+                        rhs_scale=scales[kind][:, lo : lo + 256],
+                        start=(G == 0),
+                        stop=(G == 1),
+                    )
+
+        add_ps = {}
+        gate_ps = {}
+
+        def first_half_products(kind, I):
+            if kind == "e":
+                o_ps = bank(I % 2, [P, CHUNK], F32, "o_e%d" % I)
+                second_matmul(o_ps, kind, I)
+                nc.scalar.activation(
+                    out=gate_sb[:, CHUNK * I : CHUNK * (I + 1)], in_=o_ps[:], func=ACT.Sigmoid, scale=-1.0
+                )
+            else:
+                add_ps[(0, I)] = bank(ADD_BANK[I], [P, CHUNK], F32, "o_a%d" % I)
+                second_matmul(add_ps[(0, I)], kind, I)
+
+        def second_half_gate(I):
+            z_ps = bank(7, [P, 4, P], F32, "zt%d" % I)
+            for jj in range(4):
+                for G in range(2):
+                    lo = 512 * (2 * I + jj // 2) + 256 * G + 128 * (jj % 2)
+                    nc.tensor.matmul_mx(
+                        out=z_ps[:, jj, :],
+                        lhsT=words["e"][:, lo : lo + 128].bitcast(FP8X4),
+                        lhsT_scale=scales["e"][:, lo : lo + 128],
+                        rhs=proj_words[:, 128 * G : 128 * (G + 1)].bitcast(FP8X4),
+                        rhs_scale=proj_scales[:, 128 * G : 128 * (G + 1)],
+                        start=(G == 0),
+                        stop=(G == 1),
+                    )
+            nc.scalar.activation(
+                out=gate_sb[:, CHUNK * I : CHUNK * (I + 1)],
+                in_=z_ps[:].rearrange("p j b -> p (j b)"),
+                func=ACT.Sigmoid,
+                scale=-1.0,
+            )
+            gate_ps[I] = bank(I, [P, CHUNK], F32, "gps%d" % I)
+            for jj in range(4):
+                lo = CHUNK * I + 128 * jj
+                nc.tensor.transpose(gate_ps[I][:, 128 * jj : 128 * (jj + 1)], gate_sb[:, lo : lo + 128], ident_f[:])
+
+        y_tile = {}
+
+        def y_row(half, l):
+            return y_tile[(half, l // 2)][:, D * (l % 2) : D * (l % 2 + 1)]
+
+        def multiply(half, k, I):
+            if (half, k) not in y_tile:
+                y_tile[(half, k)] = slots.tile(
+                    [P, 2 * D], F32, tag="slot%d" % SLOT_OF["y%d%d" % (half, k)], name="y%d_%d" % (half, k)
+                )
+            ns = slice(CHUNK * I, CHUNK * (I + 1))
+            yv = y_tile[(half, k)][:].rearrange("p (l n) -> p l n", l=2)
+            mv = mem_sb[half][:].rearrange("p (l n) -> p l n", l=ROWS)
+            nc.vector.tensor_tensor(
+                out=yv[:, :, ns],
+                in0=mv[:, 2 * k : 2 * k + 2, ns],
+                in1=(gate_sb[:, ns] if half == 0 else gate_ps[I][:]).unsqueeze(1).to_broadcast([P, 2, CHUNK]),
+                op=ALU.mult,
+            )
+
+        def add(half, l, I):
+            ym = y_row(half, l)[:, CHUNK * I : CHUNK * (I + 1)]
+            nc.vector.scalar_tensor_tensor(
+                out=ym,
+                in0=ym,
+                scalar=1.0,
+                in1=add_ps[(half, I)][:],
+                op0=ALU.mult,
+                op1=ALU.add,
+                accum_out=part_sums[:, ROWS * half + l, I : I + 1],
+            )
+
+        def total(first, count):
+            nc.vector.tensor_reduce(
+                out=neg_sum[:, first : first + count],
+                in_=part_sums[:, first : first + count, :],
+                axis=mybir.AxisListType.X,
+                op=ALU.add,
+                negate=True,
+            )
+
+        def add_chunk(I):
+            for l in range(ROWS):
+                add(0, l, I)
+            if I == 3:
+                total(0, ROWS)
+
+        def add_row(l):
+            for I in range(4):
+                add(1, l, I)
+            total(ROWS + l, 1)
+
+        def finish(half, l):
+            j = ROWS * half + l
+            col = slice(j, j + 1)
+            ym = y_row(half, l)
+            hbm_rows = slice(P * half, P * (half + 1))
+            nc.scalar.activation(
+                out=squares[:], in_=ym, func=ACT.Square, bias=neg_sum[:, col], scale=float(D), accum_out=sq_sum[:, col]
+            )
+            nc.scalar.activation(out=neg_mean[:, col], in_=neg_sum[:, col], func=ACT.Copy, scale=1.0 / D)
+            nc.gpsimd.tensor_scalar(
+                out=var_eps[:, col],
+                in0=sq_sum[:, col],
+                scalar1=1.0 / (D * D * D),
+                scalar2=LN_EPS,
+                op0=ALU.mult,
+                op1=ALU.add,
+            )
+            nc.gpsimd.tensor_tensor(out=rstd[:, col], in0=var_eps[:, col], in1=minus_half[:], op=ALU.pow)
+            if j >= 2 * ROWS - 2:
+                w = D // LAST_PIECES
+                for z in range(LAST_PIECES):
+                    yz = ym[:, w * z : w * (z + 1)]
+                    nc.vector.tensor_scalar(
+                        out=yz, in0=yz, scalar1=neg_mean[:, col], scalar2=rstd[:, col], op0=ALU.add, op1=ALU.mult
+                    )
+                    nc.sync.dma_start(out=out_v[hbm_rows, D * l + w * z : D * l + w * (z + 1)], in_=yz)
+            else:
+                nc.gpsimd.tensor_scalar(
+                    out=ym, in0=ym, scalar1=neg_mean[:, col], scalar2=rstd[:, col], op0=ALU.add, op1=ALU.mult
+                )
+                nc.sync.dma_start(out=out_v[hbm_rows, D * l : D * (l + 1)], in_=ym)
+
+        for j in range(4):
+            prepare_key(j, 0)
+            prepare_key(j, 1)
+        for T in range(4):
+            mean_chunk(T)
+            if T % 2 == 1:
+                if T == 1:
+                    load("m", 0)
+                    load("m", 1)
+                load("a", T - 1)
+                load("a", T)
+        quantise_waiting(0)
+        mean_out(0)
+        for step in range(2):
+            prepare(step)
+            quantise_waiting(1)
+        first_matmul(0, 0)
+        proj_out(0)
+        quantise_waiting(0)
+        first_matmul(0, 1)
+        proj_out(1)
+
+        for step in range(2, STEPS + 2):
+            if step < STEPS:
+                prepare(step)
+                quantise_waiting(1)
+            else:
+                quantise_waiting(0)
+            if step % 2 == 1:
+                kind, I = chunks[(step - 3) // 2]
+                first_half_products(kind, I)
+            if step >= STEPS - 2:
+                mean_chunk(step - STEPS + 6)
+            if 4 <= step < 12:
+                multiply(0, step % 2, (step - 4) // 2)
+            if step == 12:
+                add_chunk(0)
+
+        add_chunk(1)
+        mean_out(1)
+        first_matmul(1, 0)
+        first_matmul(1, 1)
+        add_chunk(2)
+        proj_out(0)
+        proj_out(1)
+        add_chunk(3)
+        second_half_gate(0)
+        second_half_gate(1)
+        finish(0, 0)
+        second_half_gate(2)
+        finish(0, 1)
+        second_half_gate(3)
+        finish(0, 2)
+        finish(0, 3)
+        for I in range(4):
+            add_ps[(1, I)] = bank(4 + I, [P, CHUNK], F32, "a1_%d" % I)
+            second_matmul(add_ps[(1, I)], "a", I)
+        for I in range(4):
+            multiply(1, 0, I)
+            multiply(1, 1, I)
+        add_row(0)
+        for l in range(ROWS):
+            if l + 1 < ROWS:
+                add_row(l + 1)
+            finish(1, l)

@@ -109,8 +109,6 @@ def tile_ultralightweightmemory_pa_kernel(
 
         ident_f = const.tile([P, P], F32)
         masks.make_identity(nc, ident_f[:])
-        ident_b = const.tile([P, P], BF16)
-        masks.make_identity(nc, ident_b[:])
         member = const.tile([P, 16], F32)
         nc.vector.tensor_reduce(
             out=member[:], in_=ident_f[:].rearrange("p (n s) -> p n s", s=8), axis=mybir.AxisListType.X, op=ALU.add
@@ -143,18 +141,20 @@ def tile_ultralightweightmemory_pa_kernel(
             return bank(8 - banks + turn["n"] % banks, shape, dtype, name)
 
         def prepare_key(j, e):
-            loaded = raw[("k", j)]
+            loaded = raw[("k", j)].bitcast(F32)
             ce = 2 * j + e
             group = grouped.tile([P, 2048], BF16, tag="grp", name="gk%d" % ce, align_bytes=64)
-            for g in range(4):
-                tp = transpose_bank([P, 4, P], BF16, "tpk%d_%d" % (ce, g))
-                for t in range(4):
-                    d0 = e * D + 512 * g
-                    nc.tensor.transpose(tp[:, t, :], loaded[:, d0 + t : d0 + 512 : 4], ident_b[:])
+            group_d_pairs = group[:].bitcast(F32)
+            for z in range(2):
+                tp = transpose_bank([P, 2, 2, P], F32, "tpk%d_%d" % (ce, z))
+                for i in range(2):
+                    for u in range(2):
+                        w0 = e * (D // 2) + 256 * (2 * z + i)
+                        nc.tensor.transpose(tp[:, i, u, :], loaded[:, w0 + u : w0 + 256 : 2], ident_f[:])
                 copy_out(
-                    "vs"[g % 2],
-                    group[:, 512 * g : 512 * (g + 1)].rearrange("p (c t) -> p c t", t=4),
-                    tp[:].rearrange("p t c -> p c t"),
+                    "vs"[z],
+                    group_d_pairs[:, 512 * z : 512 * (z + 1)].rearrange("q (i c u) -> q i c u", i=2, u=2),
+                    tp[:].rearrange("q i u c -> q i c u"),
                 )
             cols = slice(512 * ce, 512 * (ce + 1))
             waiting.append(lambda: quantise(words["k"][:, cols], scales["k"][:, cols], group[:]))

@@ -18,24 +18,41 @@ D = 2048
 ROWS = 4
 CHUNK = 512
 LN_EPS = 1e-5
-STEPS = 16
 LAST_PIECES = 4
 
-SLOT_OF = {
-    "k0": 0, "y00": 0,
-    "k1": 1, "y01": 1,
-    "x0": 2, "a0": 2, "y10": 2,
-    "x1": 3, "a1": 3, "y11": 3,
-    "e0": 4, "x2": 4,
-    "e1": 5, "x3": 5,
-}
-ADD_BANK = [2, 3, 4, 5]
+SLOT_TILES = (
+    ("k0 k1", "a1 e3", "y10"),
+    ("x0 x1", "a2 a3", "y11"),
+    ("x2 x3", "y00"),
+    ("k2 k3", "y01"),
+    ("e0 e1", "x4 x5"),
+    ("a0 e2", "x6 x7"),
+)
+ORDER = (("e", 0), ("e", 1), ("a", 0), ("e", 2), ("a", 1), ("e", 3), ("a", 2), ("a", 3))
+ON_SCALAR = ((0, 3),)
+ON_VECTOR = ((1, 1), (1, 2), (1, 3))
+MEAN_BANKS = (0, 1, 1, 4)
+PROJ_BANKS = ((2, 3), (0, 1))
+Z_BANKS = (7, 1)
+GATE_BANKS = (4, 5, 6, 0)
+ADD_BANKS = (1, 2, 3, 7)
+STEP_MEAN = {8: 4, 10: 5, 12: 6, 13: 7}
+MEAN_ENG = "ss"
+STEP_MULT = {3: [(0, 0)], 4: [(1, 0)], 5: [(0, 1)], 6: [(1, 1)], 9: [(0, 2)], 10: [(1, 2)], 13: [(0, 3)], 14: [(1, 3)]}
+STEP_ADD = {7: [(0, 0), (1, 0)], 8: [(2, 0), (3, 0)], 11: [(0, 1), (1, 1)], 12: [(2, 1), (3, 1)], 15: [(0, 2), (1, 2)], 16: [(2, 2), (3, 2)]}
+LOADS = "k0 k1 x0 x1 x2 x3 k2 k3 e0 m0 e1 m1 a0 e2 a1 x4 e3 x5 a2 x6 x7 a3 m2 m3".split()
 
 
 def tile_ultralightweightmemory_pa_kernel(
     tc, interface, memory, W_write_key, W_write_erase, W_write_add, out
 ):
     nc = tc.nc
+    slot_of = {}
+    for number, tiles in enumerate(SLOT_TILES):
+        for names in tiles:
+            for part, name in enumerate(names.split()):
+                slot_of[name] = (number, part, names)
+
     with ExitStack() as ctx:
         const = ctx.enter_context(tc.tile_pool(name="const", bufs=1))
         keep = ctx.enter_context(tc.tile_pool(name="keep", bufs=1))
@@ -76,22 +93,26 @@ def tile_ultralightweightmemory_pa_kernel(
         sq_sum = keep.tile([P, 2 * ROWS], F32)
         var_eps = keep.tile([P, 2 * ROWS], F32)
         rstd = keep.tile([P, 2 * ROWS], F32)
+        shift = keep.tile([P, 2 * ROWS], F32)
         table_warm = keep.tile([P, 1], F32)
 
         raw = {}
         slot_tile = {}
 
-        def load(kind, idx):
+        def slot(name, shape, dtype):
+            return slots.tile(shape, dtype, tag="slot%d" % slot_of[name][0], name="slot_%s" % name)
+
+        for load in LOADS:
+            kind, idx = load[0], int(load[1])
             if kind == "m":
                 half, part = divmod(idx, 2)
                 cols = slice(2 * D * part, 2 * D * (part + 1))
                 nc.sync.dma_start(out=mem_sb[half][:, cols], in_=mem_v[P * half : P * (half + 1), cols])
-                return
-            if idx % 2 == 0:
-                slot_tile[(kind, idx // 2)] = slots.tile(
-                    [P, 8192], BF16, tag="slot%d" % SLOT_OF["%s%d" % (kind, idx // 2)], name="raw_%s%d" % (kind, idx // 2)
-                )
-            t = slot_tile[(kind, idx // 2)][:, 4096 * (idx % 2) : 4096 * (idx % 2 + 1)]
+                continue
+            tile_name = slot_of[load][2]
+            if tile_name not in slot_tile:
+                slot_tile[tile_name] = slot(load, [P, 8192], BF16)
+            t = slot_tile[tile_name][:, 4096 * slot_of[load][1] : 4096 * (slot_of[load][1] + 1)]
             if kind == "k":
                 nc.sync.dma_start(out=t, in_=wk_v[idx // 2, idx % 2])
             elif kind == "x":
@@ -99,13 +120,6 @@ def tile_ultralightweightmemory_pa_kernel(
             else:
                 nc.sync.dma_start(out=t.rearrange("p (h x) -> p h x", h=2), in_=w2_v[kind][idx])
             raw[(kind, idx)] = t
-
-        for i in range(4):
-            load("k", i)
-        for i in range(4):
-            load("x", i)
-        for i in range(4):
-            load("e", i)
 
         ident_f = const.tile([P, P], F32)
         masks.make_identity(nc, ident_f[:])
@@ -130,15 +144,15 @@ def tile_ultralightweightmemory_pa_kernel(
 
         waiting = []
 
-        def quantise_waiting(keep_back):
-            while len(waiting) > keep_back:
+        def quantise_waiting(count):
+            for i in range(count):
                 waiting.pop(0)()
 
         turn = {"n": 0}
 
-        def transpose_bank(shape, dtype, name, banks=4):
+        def transpose_bank(name, banks=3):
             turn["n"] += 1
-            return bank(8 - banks + turn["n"] % banks, shape, dtype, name)
+            return bank(8 - banks + turn["n"] % banks, [P, 2, 2, P], F32, name)
 
         def prepare_key(j, e):
             loaded = raw[("k", j)].bitcast(F32)
@@ -146,7 +160,7 @@ def tile_ultralightweightmemory_pa_kernel(
             group = grouped.tile([P, 2048], BF16, tag="grp", name="gk%d" % ce, align_bytes=64)
             group_d_pairs = group[:].bitcast(F32)
             for z in range(2):
-                tp = transpose_bank([P, 2, 2, P], F32, "tpk%d_%d" % (ce, z))
+                tp = transpose_bank("tpk%d_%d" % (ce, z), 4)
                 for i in range(2):
                     for u in range(2):
                         w0 = e * (D // 2) + 256 * (2 * z + i)
@@ -158,44 +172,44 @@ def tile_ultralightweightmemory_pa_kernel(
                 )
             cols = slice(512 * ce, 512 * (ce + 1))
             waiting.append(lambda: quantise(words["k"][:, cols], scales["k"][:, cols], group[:]))
-            quantise_waiting(1)
 
         mean_ps = {}
 
         def mean_chunk(T):
-            half, Tl = divmod(T, 4)
-            if Tl == 0:
-                mean_ps[half] = [bank(z, [P, 8, 64], F32, "mean%d_%d" % (half, z)) for z in range(2)]
+            if T % 2 == 0:
+                mean_ps[T // 2] = bank(MEAN_BANKS[T // 2], [P, 16, 32], F32, "mean%d" % T)
             xt = raw[("x", T)]
             for c in range(16):
                 for i in range(2):
                     lo = i * D + 512 * (c // 4)
                     nc.tensor.matmul(
-                        mean_ps[half][c // 8][:, c % 8, 16 * Tl : 16 * (Tl + 1)],
+                        mean_ps[T // 2][:, c, 16 * (T % 2) : 16 * (T % 2 + 1)],
                         lhsT=xt[:, lo + c % 4 : lo + 512 : 4],
                         rhs=averager[:],
                         start=(i == 0),
                         stop=(i == 1),
                     )
 
-        def mean_out(half):
-            for z in range(2):
-                for g in (z, 2 + z):
-                    src = mean_ps[half][g // 2][:, 4 * (g % 2) : 4 * (g % 2) + 4, :]
-                    copy_out(
-                        "vs"[g // 2],
-                        mean_bf[:, 512 * g : 512 * (g + 1)].rearrange("p (b u t) -> p b u t", u=2, t=4),
-                        src.rearrange("p t b -> p b t").unsqueeze(2).to_broadcast([P, 64, 2, 4]),
-                    )
+        def mean_out(pair, engine):
+            for g in range(4):
+                lo = 512 * g + 256 * (pair % 2)
+                copy_out(
+                    engine,
+                    mean_bf[:, lo : lo + 256].rearrange("p (b u t) -> p b u t", u=2, t=4),
+                    mean_ps[pair][:, 4 * g : 4 * g + 4, :].rearrange("p t b -> p b t").unsqueeze(2).to_broadcast([P, 32, 2, 4]),
+                )
+
+        def mean_quantise():
             quantise(mean_words[:, 0:256], mean_scales[:, 0:256], mean_bf[:, 0:1024])
             quantise(mean_words[:, 256:512], mean_scales[:, 256:512], mean_bf[:, 1024:2048])
 
         proj_ps = {}
 
-        def first_matmul(half, G):
-            pj = bank(2 + 4 * half + G, [P, 4, P], F32, "pj%d_%d" % (half, G))
-            proj_ps[G] = pj
-            for t in range(4):
+        def first_matmul(half, G, ts):
+            if ts[0] == 0:
+                proj_ps[G] = bank(PROJ_BANKS[half][G], [P, 4, P], F32, "pj%d_%d" % (half, G))
+            pj = proj_ps[G]
+            for t in ts:
                 ce = 4 * G + t
                 for g in range(4):
                     lo = 512 * ce + 128 * g
@@ -209,25 +223,24 @@ def tile_ultralightweightmemory_pa_kernel(
                         stop=(g == 3),
                     )
 
-        def proj_out(G):
+        def proj_out(G, engine):
             copy_out(
-                "v",
+                engine,
                 proj_bf[:, 512 * G : 512 * (G + 1)].rearrange("p (b t) -> p b t", t=4),
                 proj_ps[G][:].rearrange("p t b -> p b t"),
             )
+
+        def proj_quantise(G):
             cols = slice(128 * G, 128 * (G + 1))
             quantise(proj_words[:, cols], proj_scales[:, cols], proj_bf[:, 512 * G : 512 * (G + 1)])
 
-        chunks = [("e", I) for I in range(4)] + [("a", I) for I in range(4)]
-
-        def prepare(step):
-            kind, I = chunks[step // 2]
-            h = step % 2
+        def prepare(chunk, h):
+            kind, I = chunk
             r_pairs = raw[(kind, I)].bitcast(F32)
-            group = grouped.tile([P, 2048], BF16, tag="grp", name="gw%d" % step, align_bytes=64)
+            group = grouped.tile([P, 2048], BF16, tag="grp", name="g%s%d%d" % (kind, I, h), align_bytes=64)
             group_r_pairs = group[:].bitcast(F32)
             for G in range(2):
-                tp = transpose_bank([P, 2, 2, P], F32, "tpw%d_%d" % (step, G), 2 if step >= STEPS - 2 else 4)
+                tp = transpose_bank("tp%s%d%d%d" % (kind, I, h, G))
                 for c in range(2):
                     for u in range(2):
                         w0 = (h * 2 + c) * 512 + 256 * G
@@ -237,12 +250,6 @@ def tile_ultralightweightmemory_pa_kernel(
                     group_r_pairs[:, 512 * G : 512 * (G + 1)].rearrange("q (p c u) -> q p c u", c=2, u=2),
                     tp[:].rearrange("q c u p -> q p c u"),
                 )
-            if kind == "e" and step % 4 == 3:
-                load("x", 3 + I)
-                load("x", 4 + I)
-                if I == 3:
-                    load("m", 2)
-                    load("m", 3)
             cols = slice(512 * (2 * I + h), 512 * (2 * I + h + 1))
             waiting.append(lambda: quantise(words[kind][:, cols], scales[kind][:, cols], group[:]))
 
@@ -263,24 +270,27 @@ def tile_ultralightweightmemory_pa_kernel(
         add_ps = {}
         gate_ps = {}
 
-        def first_half_products(kind, I):
+        def first_half_products(chunk):
+            kind, I = chunk
             if kind == "e":
-                o_ps = bank(I % 2, [P, CHUNK], F32, "o_e%d" % I)
+                o_ps = bank(0, [P, CHUNK], F32, "o_e%d" % I)
                 second_matmul(o_ps, kind, I)
                 nc.scalar.activation(
                     out=gate_sb[:, CHUNK * I : CHUNK * (I + 1)], in_=o_ps[:], func=ACT.Sigmoid, scale=-1.0
                 )
             else:
-                add_ps[(0, I)] = bank(ADD_BANK[I], [P, CHUNK], F32, "o_a%d" % I)
+                add_ps[(0, I)] = bank(2 + I % 2, [P, CHUNK], F32, "o_a%d" % I)
                 second_matmul(add_ps[(0, I)], kind, I)
 
-        def second_half_gate(I):
-            z_ps = bank(7, [P, 4, P], F32, "zt%d" % I)
+        z_ps = {}
+
+        def second_half_z(I):
+            z_ps[I] = bank(Z_BANKS[I % 2], [P, 4, P], F32, "zt%d" % I)
             for jj in range(4):
                 for G in range(2):
                     lo = 512 * (2 * I + jj // 2) + 256 * G + 128 * (jj % 2)
                     nc.tensor.matmul_mx(
-                        out=z_ps[:, jj, :],
+                        out=z_ps[I][:, jj, :],
                         lhsT=words["e"][:, lo : lo + 128].bitcast(FP8X4),
                         lhsT_scale=scales["e"][:, lo : lo + 128],
                         rhs=proj_words[:, 128 * G : 128 * (G + 1)].bitcast(FP8X4),
@@ -288,13 +298,15 @@ def tile_ultralightweightmemory_pa_kernel(
                         start=(G == 0),
                         stop=(G == 1),
                     )
+
+        def second_half_gate(I):
             nc.scalar.activation(
                 out=gate_sb[:, CHUNK * I : CHUNK * (I + 1)],
-                in_=z_ps[:].rearrange("p j b -> p (j b)"),
+                in_=z_ps[I][:].rearrange("p j b -> p (j b)"),
                 func=ACT.Sigmoid,
                 scale=-1.0,
             )
-            gate_ps[I] = bank(I, [P, CHUNK], F32, "gps%d" % I)
+            gate_ps[I] = bank(GATE_BANKS[I], [P, CHUNK], F32, "gps%d" % I)
             for jj in range(4):
                 lo = CHUNK * I + 128 * jj
                 nc.tensor.transpose(gate_ps[I][:, 128 * jj : 128 * (jj + 1)], gate_sb[:, lo : lo + 128], ident_f[:])
@@ -306,9 +318,7 @@ def tile_ultralightweightmemory_pa_kernel(
 
         def multiply(half, k, I):
             if (half, k) not in y_tile:
-                y_tile[(half, k)] = slots.tile(
-                    [P, 2 * D], F32, tag="slot%d" % SLOT_OF["y%d%d" % (half, k)], name="y%d_%d" % (half, k)
-                )
+                y_tile[(half, k)] = slot("y%d%d" % (half, k), [P, 2 * D], F32)
             ns = slice(CHUNK * I, CHUNK * (I + 1))
             yv = y_tile[(half, k)][:].rearrange("p (l n) -> p l n", l=2)
             mv = mem_sb[half][:].rearrange("p (l n) -> p l n", l=ROWS)
@@ -351,13 +361,16 @@ def tile_ultralightweightmemory_pa_kernel(
                 add(1, l, I)
             total(ROWS + l, 1)
 
-        def finish(half, l):
+        def statistics(half, l):
             j = ROWS * half + l
             col = slice(j, j + 1)
-            ym = y_row(half, l)
-            hbm_rows = slice(P * half, P * (half + 1))
             nc.scalar.activation(
-                out=squares[:], in_=ym, func=ACT.Square, bias=neg_sum[:, col], scale=float(D), accum_out=sq_sum[:, col]
+                out=squares[:],
+                in_=y_row(half, l),
+                func=ACT.Square,
+                bias=neg_sum[:, col],
+                scale=float(D),
+                accum_out=sq_sum[:, col],
             )
             nc.scalar.activation(out=neg_mean[:, col], in_=neg_sum[:, col], func=ACT.Copy, scale=1.0 / D)
             nc.gpsimd.tensor_scalar(
@@ -369,7 +382,18 @@ def tile_ultralightweightmemory_pa_kernel(
                 op1=ALU.add,
             )
             nc.gpsimd.tensor_tensor(out=rstd[:, col], in0=var_eps[:, col], in1=minus_half[:], op=ALU.pow)
-            if j >= 2 * ROWS - 2:
+            if (half, l) in ON_SCALAR:
+                nc.gpsimd.tensor_tensor(out=shift[:, col], in0=neg_mean[:, col], in1=rstd[:, col], op=ALU.mult)
+
+        def normalise(half, l):
+            j = ROWS * half + l
+            col = slice(j, j + 1)
+            ym = y_row(half, l)
+            hbm_rows = slice(P * half, P * (half + 1))
+            if (half, l) in ON_SCALAR:
+                nc.scalar.activation(out=ym, in_=ym, func=ACT.Identity, bias=shift[:, col], scale=rstd[:, col])
+                nc.sync.dma_start(out=out_v[hbm_rows, D * l : D * (l + 1)], in_=ym)
+            elif (half, l) in ON_VECTOR:
                 w = D // LAST_PIECES
                 for z in range(LAST_PIECES):
                     yz = ym[:, w * z : w * (z + 1)]
@@ -383,68 +407,95 @@ def tile_ultralightweightmemory_pa_kernel(
                 )
                 nc.sync.dma_start(out=out_v[hbm_rows, D * l : D * (l + 1)], in_=ym)
 
-        for j in range(4):
-            prepare_key(j, 0)
-            prepare_key(j, 1)
-        for T in range(4):
-            mean_chunk(T)
-            if T % 2 == 1:
-                if T == 1:
-                    load("m", 0)
-                    load("m", 1)
-                load("a", T - 1)
-                load("a", T)
-        quantise_waiting(0)
-        mean_out(0)
-        for step in range(2):
-            prepare(step)
-            quantise_waiting(1)
-        first_matmul(0, 0)
-        proj_out(0)
-        quantise_waiting(0)
-        first_matmul(0, 1)
-        proj_out(1)
-
-        for step in range(2, STEPS + 2):
-            if step < STEPS:
-                prepare(step)
+        for ce in range(4):
+            prepare_key(ce // 2, ce % 2)
+            if ce > 0:
                 quantise_waiting(1)
-            else:
-                quantise_waiting(0)
-            if step % 2 == 1:
-                kind, I = chunks[(step - 3) // 2]
-                first_half_products(kind, I)
-            if step >= STEPS - 2:
-                mean_chunk(step - STEPS + 6)
-            if 4 <= step < 12:
-                multiply(0, step % 2, (step - 4) // 2)
-            if step == 12:
-                add_chunk(0)
-
-        add_chunk(1)
-        mean_out(1)
-        first_matmul(1, 0)
-        first_matmul(1, 1)
+        mean_chunk(0)
+        quantise_waiting(1)
+        mean_chunk(1)
+        mean_out(0, "s")
+        mean_chunk(2)
+        mean_chunk(3)
+        mean_out(1, "v")
+        mean_quantise()
+        for ce in range(4, 8):
+            prepare_key(ce // 2, ce % 2)
+            if ce > 4:
+                quantise_waiting(1)
+        prepare(ORDER[0], 0)
+        quantise_waiting(1)
+        prepare(ORDER[0], 1)
+        first_matmul(0, 0, range(4))
+        quantise_waiting(1)
+        first_matmul(0, 1, range(4))
+        proj_out(0, "v")
+        quantise_waiting(1)
+        proj_quantise(0)
+        proj_out(1, "v")
+        proj_quantise(1)
+        for step in range(2, 15):
+            prepare(ORDER[step // 2], step % 2)
+            if step in STEP_MEAN:
+                mean_chunk(STEP_MEAN[step])
+            if step in (11, 13):
+                mean_out(2 + step // 13, "s")
+            if step >= 3:
+                quantise_waiting(1)
+            if step % 2 == 0:
+                first_half_products(ORDER[(step - 2) // 2])
+            for k, I in STEP_MULT.get(step, ()):
+                multiply(0, k, I)
+            for l, I in STEP_ADD.get(step, ()):
+                add(0, l, I)
+        prepare(ORDER[7], 1)
+        mean_quantise()
+        first_matmul(1, 0, range(4))
+        first_matmul(1, 1, range(4))
+        quantise_waiting(1)
+        proj_out(0, "s")
+        proj_out(1, "s")
         add_chunk(2)
-        proj_out(0)
-        proj_out(1)
+        quantise_waiting(1)
+        first_half_products(ORDER[7])
+        proj_quantise(0)
+        proj_quantise(1)
+        second_half_z(0)
+        second_half_z(1)
         add_chunk(3)
         second_half_gate(0)
+        second_half_z(2)
         second_half_gate(1)
-        finish(0, 0)
+        statistics(0, 0)
+        normalise(0, 0)
+        second_half_z(3)
         second_half_gate(2)
-        finish(0, 1)
+        statistics(0, 1)
+        normalise(0, 1)
         second_half_gate(3)
-        finish(0, 2)
-        finish(0, 3)
         for I in range(4):
-            add_ps[(1, I)] = bank(4 + I, [P, CHUNK], F32, "a1_%d" % I)
+            add_ps[(1, I)] = bank(ADD_BANKS[I], [P, CHUNK], F32, "a1_%d" % I)
             second_matmul(add_ps[(1, I)], "a", I)
-        for I in range(4):
+        for I in range(2):
             multiply(1, 0, I)
             multiply(1, 1, I)
+        for I in range(2, 4):
+            multiply(1, 0, I)
+        statistics(0, 2)
+        statistics(0, 3)
+        normalise(0, 2)
         add_row(0)
-        for l in range(ROWS):
-            if l + 1 < ROWS:
-                add_row(l + 1)
-            finish(1, l)
+        normalise(0, 3)
+        add_row(1)
+        statistics(1, 0)
+        normalise(1, 0)
+        for I in range(2, 4):
+            multiply(1, 1, I)
+        statistics(1, 1)
+        add_row(2)
+        statistics(1, 2)
+        add_row(3)
+        normalise(1, 1)
+        normalise(1, 2)
+        statistics(1, 3)
+        normalise(1, 3)

@@ -30,17 +30,17 @@ SLOT_TILES = (
 )
 ORDER = (("e", 0), ("e", 1), ("a", 0), ("e", 2), ("a", 1), ("e", 3), ("a", 2), ("a", 3))
 ON_SCALAR = ((0, 3),)
-ON_VECTOR = ((1, 1), (1, 2), (1, 3))
+ON_VECTOR = ((1, 2), (1, 3))
 MEAN_BANKS = (0, 1, 1, 4)
 PROJ_BANKS = ((2, 3), (0, 1))
 Z_BANKS = (7, 1)
 GATE_BANKS = (4, 5, 6, 0)
-ADD_BANKS = (1, 2, 3, 7)
+ADD_BANKS = (2, 3, 7, 1)
 STEP_MEAN = {8: 4, 10: 5, 12: 6, 13: 7}
 MEAN_ENG = "ss"
 STEP_MULT = {3: [(0, 0)], 4: [(1, 0)], 5: [(0, 1)], 6: [(1, 1)], 9: [(0, 2)], 10: [(1, 2)], 13: [(0, 3)], 14: [(1, 3)]}
 STEP_ADD = {7: [(0, 0), (1, 0)], 8: [(2, 0), (3, 0)], 11: [(0, 1), (1, 1)], 12: [(2, 1), (3, 1)], 15: [(0, 2), (1, 2)], 16: [(2, 2), (3, 2)]}
-LOADS = "k0 k1 x0 x1 x2 x3 k2 k3 e0 m0 e1 m1 a0 e2 a1 x4 e3 x5 a2 x6 x7 a3 m2 m3".split()
+LOADS = "k0 k1 x0 x1 x2 x3 k2 e0 k3 e1 m0 a0 m1 e2 a1 x4 e3 x5 x6 x7 a2 a3 m2 m3".split()
 
 
 def tile_ultralightweightmemory_pa_kernel(
@@ -57,7 +57,7 @@ def tile_ultralightweightmemory_pa_kernel(
         const = ctx.enter_context(tc.tile_pool(name="const", bufs=1))
         keep = ctx.enter_context(tc.tile_pool(name="keep", bufs=1))
         slots = ctx.enter_context(tc.tile_pool(name="slots", bufs=1))
-        grouped = ctx.enter_context(tc.tile_pool(name="grouped", bufs=4))
+        grouped = ctx.enter_context(tc.tile_pool(name="grouped", bufs=6))
         psum = ctx.enter_context(tc.psum_pool(name="psum", bufs=1))
         ctx.enter_context(tc.manual_schedule())
 
@@ -91,7 +91,10 @@ def tile_ultralightweightmemory_pa_kernel(
         neg_sum = keep.tile([P, 2 * ROWS], F32)
         neg_mean = keep.tile([P, 2 * ROWS], F32)
         sq_sum = keep.tile([P, 2 * ROWS], F32)
-        var_eps = keep.tile([P, 2 * ROWS], F32)
+        neg_c = keep.tile([P, ROWS], F32)
+        sq_parts = keep.tile([P, ROWS, 3], F32)
+        offset = keep.tile([P, ROWS], F32)
+        var = keep.tile([P, ROWS], F32)
         rstd = keep.tile([P, 2 * ROWS], F32)
         shift = keep.tile([P, 2 * ROWS], F32)
         table_warm = keep.tile([P, 1], F32)
@@ -311,6 +314,10 @@ def tile_ultralightweightmemory_pa_kernel(
                 lo = CHUNK * I + 128 * jj
                 nc.tensor.transpose(gate_ps[I][:, 128 * jj : 128 * (jj + 1)], gate_sb[:, lo : lo + 128], ident_f[:])
 
+        def second_half_add(I):
+            add_ps[(1, I)] = bank(ADD_BANKS[I], [P, CHUNK], F32, "a1_%d" % I)
+            second_matmul(add_ps[(1, I)], "a", I)
+
         y_tile = {}
 
         def y_row(half, l):
@@ -361,6 +368,41 @@ def tile_ultralightweightmemory_pa_kernel(
                 add(1, l, I)
             total(ROWS + l, 1)
 
+        def squares_of(l, first, last):
+            if (l, first) == (0, 0):
+                nc.scalar.activation(out=neg_c[:], in_=part_sums[:, 0:ROWS, 0], func=ACT.Copy, scale=-1.0 / CHUNK)
+            ns = slice(CHUNK * first, CHUNK * last)
+            part = min(first, 2)
+            nc.scalar.activation(
+                out=squares[:, ns],
+                in_=y_row(0, l)[:, ns],
+                func=ACT.Square,
+                bias=neg_c[:, l : l + 1],
+                accum_out=sq_parts[:, l, part : part + 1],
+            )
+
+        def first_half_statistics(first):
+            rows = slice(first, first + 2)
+            nc.scalar.activation(out=neg_mean[:, rows], in_=neg_sum[:, rows], func=ACT.Copy, scale=1.0 / D)
+            nc.gpsimd.tensor_tensor(out=offset[:, rows], in0=neg_mean[:, rows], in1=neg_c[:, rows], op=ALU.subtract)
+            nc.gpsimd.tensor_tensor(out=offset[:, rows], in0=offset[:, rows], in1=offset[:, rows], op=ALU.mult)
+            nc.gpsimd.tensor_tensor(
+                out=var[:, rows], in0=sq_parts[:, rows, 0], in1=sq_parts[:, rows, 1], op=ALU.add
+            )
+            nc.gpsimd.tensor_tensor(out=var[:, rows], in0=var[:, rows], in1=sq_parts[:, rows, 2], op=ALU.add)
+            nc.gpsimd.tensor_scalar(
+                out=var[:, rows], in0=var[:, rows], scalar1=1.0 / D, scalar2=LN_EPS, op0=ALU.mult, op1=ALU.add
+            )
+            nc.gpsimd.tensor_tensor(out=var[:, rows], in0=var[:, rows], in1=offset[:, rows], op=ALU.subtract)
+            if first == 0:
+                nc.gpsimd.tensor_tensor(
+                    out=rstd[:, rows], in0=var[:, rows], in1=minus_half[:].to_broadcast([P, 2]), op=ALU.pow
+                )
+            else:
+                nc.scalar.activation(out=rstd[:, rows], in_=var[:, rows], func=ACT.Abs_reciprocal_sqrt)
+            if first == 2:
+                nc.gpsimd.tensor_tensor(out=shift[:, rows], in0=neg_mean[:, rows], in1=rstd[:, rows], op=ALU.mult)
+
         def statistics(half, l):
             j = ROWS * half + l
             col = slice(j, j + 1)
@@ -372,18 +414,14 @@ def tile_ultralightweightmemory_pa_kernel(
                 scale=float(D),
                 accum_out=sq_sum[:, col],
             )
-            nc.scalar.activation(out=neg_mean[:, col], in_=neg_sum[:, col], func=ACT.Copy, scale=1.0 / D)
-            nc.gpsimd.tensor_scalar(
-                out=var_eps[:, col],
-                in0=sq_sum[:, col],
-                scalar1=1.0 / (D * D * D),
-                scalar2=LN_EPS,
-                op0=ALU.mult,
-                op1=ALU.add,
+            nc.scalar.activation(
+                out=rstd[:, col],
+                in_=sq_sum[:, col],
+                func=ACT.Abs_reciprocal_sqrt,
+                bias=LN_EPS,
+                scale=1.0 / (D * D * D),
             )
-            nc.gpsimd.tensor_tensor(out=rstd[:, col], in0=var_eps[:, col], in1=minus_half[:], op=ALU.pow)
-            if (half, l) in ON_SCALAR:
-                nc.gpsimd.tensor_tensor(out=shift[:, col], in0=neg_mean[:, col], in1=rstd[:, col], op=ALU.mult)
+            nc.scalar.activation(out=neg_mean[:, col], in_=neg_sum[:, col], func=ACT.Copy, scale=1.0 / D)
 
         def normalise(half, l):
             j = ROWS * half + l
@@ -419,83 +457,128 @@ def tile_ultralightweightmemory_pa_kernel(
         mean_chunk(3)
         mean_out(1, "v")
         mean_quantise()
-        for ce in range(4, 8):
-            prepare_key(ce // 2, ce % 2)
-            if ce > 4:
-                quantise_waiting(1)
+        prepare_key(2, 0)
+        prepare_key(2, 1)
+        quantise_waiting(1)
         prepare(ORDER[0], 0)
         quantise_waiting(1)
         prepare(ORDER[0], 1)
+        quantise_waiting(1)
+        prepare_key(3, 0)
+        quantise_waiting(1)
+        prepare_key(3, 1)
         first_matmul(0, 0, range(4))
         quantise_waiting(1)
-        first_matmul(0, 1, range(4))
-        proj_out(0, "v")
+        first_matmul(0, 1, range(2))
         quantise_waiting(1)
-        proj_quantise(0)
+        first_matmul(0, 1, range(2, 4))
+        proj_out(0, "s")
         proj_out(1, "v")
+        proj_quantise(0)
         proj_quantise(1)
-        for step in range(2, 15):
-            prepare(ORDER[step // 2], step % 2)
-            if step in STEP_MEAN:
-                mean_chunk(STEP_MEAN[step])
-            if step in (11, 13):
-                mean_out(2 + step // 13, "s")
-            if step >= 3:
+        def unit(step):
+            j, part = divmod(step - 2 if step < 4 else step - 3, 2)
+            if step < 2 or step == 4:
+                return
+            kind, I = ORDER[j]
+            if kind == "e":
+                multiply(0, part, I)
+            else:
+                add(0, 2 * part, I)
+                add(0, 2 * part + 1, I)
+
+        for step in range(12):
+            if step + 2 < 12:
+                prepare(ORDER[(step + 2) // 2], step % 2)
+            if step == 7:
+                mean_chunk(4)
+            if step == 9:
+                mean_chunk(5)
+                mean_out(2, "s")
+            if step == 11:
+                mean_chunk(6)
+            if step >= 2:
                 quantise_waiting(1)
-            if step % 2 == 0:
-                first_half_products(ORDER[(step - 2) // 2])
-            for k, I in STEP_MULT.get(step, ()):
-                multiply(0, k, I)
-            for l, I in STEP_ADD.get(step, ()):
-                add(0, l, I)
-        prepare(ORDER[7], 1)
+            if step in (0, 4, 6, 8, 10):
+                first_half_products(ORDER[max(step // 2 - 1, 0)])
+            unit(step)
+        for l in range(ROWS):
+            squares_of(l, 0, 1)
+        first_half_products(ORDER[5])
+        mean_chunk(7)
+        mean_out(3, "s")
+        for step in range(12, 15):
+            unit(step)
+        for h in range(4):
+            prepare(ORDER[6 + h // 2], h % 2)
+        quantise_waiting(2)
+        first_half_products(ORDER[6])
+        for l in range(2):
+            squares_of(l, 1, 2)
         mean_quantise()
         first_matmul(1, 0, range(4))
         first_matmul(1, 1, range(4))
-        quantise_waiting(1)
         proj_out(0, "s")
         proj_out(1, "s")
-        add_chunk(2)
-        quantise_waiting(1)
+        quantise_waiting(2)
         first_half_products(ORDER[7])
+        add(0, 0, 2)
+        add(0, 1, 2)
         proj_quantise(0)
         proj_quantise(1)
+        for l in range(2, 4):
+            squares_of(l, 1, 2)
         second_half_z(0)
         second_half_z(1)
-        add_chunk(3)
+        add(0, 0, 3)
+        add(0, 1, 3)
+        total(0, 2)
+        for I in range(2, 4):
+            add(0, 2, I)
+            add(0, 3, I)
+        total(2, 2)
         second_half_gate(0)
         second_half_z(2)
         second_half_gate(1)
-        statistics(0, 0)
-        normalise(0, 0)
+        second_half_add(0)
+        second_half_add(1)
         second_half_z(3)
+        for l in range(2):
+            squares_of(l, 2, 4)
+        first_half_statistics(0)
+        normalise(0, 0)
         second_half_gate(2)
-        statistics(0, 1)
-        normalise(0, 1)
+        for l in range(2, 4):
+            squares_of(l, 2, 4)
         second_half_gate(3)
-        for I in range(4):
-            add_ps[(1, I)] = bank(ADD_BANKS[I], [P, CHUNK], F32, "a1_%d" % I)
-            second_matmul(add_ps[(1, I)], "a", I)
+        normalise(0, 1)
+        first_half_statistics(2)
+        normalise(0, 2)
+        normalise(0, 3)
+        second_half_add(2)
+        second_half_add(3)
         for I in range(2):
             multiply(1, 0, I)
             multiply(1, 1, I)
-        for I in range(2, 4):
-            multiply(1, 0, I)
-        statistics(0, 2)
-        statistics(0, 3)
-        normalise(0, 2)
-        add_row(0)
-        normalise(0, 3)
-        add_row(1)
+        for I in range(2):
+            add(1, 0, I)
+        multiply(1, 0, 2)
+        for I in range(2):
+            add(1, 1, I)
+        multiply(1, 0, 3)
+        for l in range(2):
+            for I in range(2, 4):
+                add(1, l, I)
+            total(ROWS + l, 1)
         statistics(1, 0)
         normalise(1, 0)
         for I in range(2, 4):
             multiply(1, 1, I)
         statistics(1, 1)
+        normalise(1, 1)
         add_row(2)
         statistics(1, 2)
         add_row(3)
-        normalise(1, 1)
         normalise(1, 2)
         statistics(1, 3)
         normalise(1, 3)

@@ -29,7 +29,6 @@ SLOT_TILES = (
     ("a0 e2", "x6 x7"),
 )
 ORDER = (("e", 0), ("e", 1), ("a", 0), ("e", 2), ("a", 1), ("e", 3), ("a", 2), ("a", 3))
-ON_SCALAR = ((0, 3),)
 ON_VECTOR = ((1, 2), (1, 3))
 MEAN_BANKS = (0, 1, 1, 4)
 PROJ_BANKS = ((2, 3), (0, 1))
@@ -40,7 +39,7 @@ STEP_MEAN = {8: 4, 10: 5, 12: 6, 13: 7}
 MEAN_ENG = "ss"
 STEP_MULT = {3: [(0, 0)], 4: [(1, 0)], 5: [(0, 1)], 6: [(1, 1)], 9: [(0, 2)], 10: [(1, 2)], 13: [(0, 3)], 14: [(1, 3)]}
 STEP_ADD = {7: [(0, 0), (1, 0)], 8: [(2, 0), (3, 0)], 11: [(0, 1), (1, 1)], 12: [(2, 1), (3, 1)], 15: [(0, 2), (1, 2)], 16: [(2, 2), (3, 2)]}
-LOADS = "k0 k1 x0 x1 x2 x3 k2 e0 k3 e1 m0 a0 m1 e2 a1 x4 e3 x5 x6 x7 a2 a3 m2 m3".split()
+LOADS = "k0 k1 x0 x1 e0 x2 x3 k2 k3 e1 m0 a0 m1 e2 a1 x4 e3 x5 x6 x7 a2 a3 m2 m3".split()
 
 
 def tile_ultralightweightmemory_pa_kernel(
@@ -91,12 +90,8 @@ def tile_ultralightweightmemory_pa_kernel(
         neg_sum = keep.tile([P, 2 * ROWS], F32)
         neg_mean = keep.tile([P, 2 * ROWS], F32)
         sq_sum = keep.tile([P, 2 * ROWS], F32)
-        neg_c = keep.tile([P, ROWS], F32)
-        sq_parts = keep.tile([P, ROWS, 3], F32)
-        offset = keep.tile([P, ROWS], F32)
         var = keep.tile([P, ROWS], F32)
         rstd = keep.tile([P, 2 * ROWS], F32)
-        shift = keep.tile([P, 2 * ROWS], F32)
         table_warm = keep.tile([P, 1], F32)
 
         raw = {}
@@ -194,12 +189,12 @@ def tile_ultralightweightmemory_pa_kernel(
                     )
 
         def mean_out(pair, engine):
-            for g in range(4):
-                lo = 512 * g + 256 * (pair % 2)
+            dst = mean_bf[:].rearrange("p (g h b u t) -> p h u g b t", g=4, h=2, u=2, t=4)
+            for u in range(2):
                 copy_out(
                     engine,
-                    mean_bf[:, lo : lo + 256].rearrange("p (b u t) -> p b u t", u=2, t=4),
-                    mean_ps[pair][:, 4 * g : 4 * g + 4, :].rearrange("p t b -> p b t").unsqueeze(2).to_broadcast([P, 32, 2, 4]),
+                    dst[:, pair % 2, u, :, :, :],
+                    mean_ps[pair][:].rearrange("p (g t) b -> p g b t", t=4),
                 )
 
         def mean_quantise():
@@ -368,41 +363,6 @@ def tile_ultralightweightmemory_pa_kernel(
                 add(1, l, I)
             total(ROWS + l, 1)
 
-        def squares_of(l, first, last):
-            if (l, first) == (0, 0):
-                nc.scalar.activation(out=neg_c[:], in_=part_sums[:, 0:ROWS, 0], func=ACT.Copy, scale=-1.0 / CHUNK)
-            ns = slice(CHUNK * first, CHUNK * last)
-            part = min(first, 2)
-            nc.scalar.activation(
-                out=squares[:, ns],
-                in_=y_row(0, l)[:, ns],
-                func=ACT.Square,
-                bias=neg_c[:, l : l + 1],
-                accum_out=sq_parts[:, l, part : part + 1],
-            )
-
-        def first_half_statistics(first):
-            rows = slice(first, first + 2)
-            nc.scalar.activation(out=neg_mean[:, rows], in_=neg_sum[:, rows], func=ACT.Copy, scale=1.0 / D)
-            nc.gpsimd.tensor_tensor(out=offset[:, rows], in0=neg_mean[:, rows], in1=neg_c[:, rows], op=ALU.subtract)
-            nc.gpsimd.tensor_tensor(out=offset[:, rows], in0=offset[:, rows], in1=offset[:, rows], op=ALU.mult)
-            nc.gpsimd.tensor_tensor(
-                out=var[:, rows], in0=sq_parts[:, rows, 0], in1=sq_parts[:, rows, 1], op=ALU.add
-            )
-            nc.gpsimd.tensor_tensor(out=var[:, rows], in0=var[:, rows], in1=sq_parts[:, rows, 2], op=ALU.add)
-            nc.gpsimd.tensor_scalar(
-                out=var[:, rows], in0=var[:, rows], scalar1=1.0 / D, scalar2=LN_EPS, op0=ALU.mult, op1=ALU.add
-            )
-            nc.gpsimd.tensor_tensor(out=var[:, rows], in0=var[:, rows], in1=offset[:, rows], op=ALU.subtract)
-            if first == 0:
-                nc.gpsimd.tensor_tensor(
-                    out=rstd[:, rows], in0=var[:, rows], in1=minus_half[:].to_broadcast([P, 2]), op=ALU.pow
-                )
-            else:
-                nc.scalar.activation(out=rstd[:, rows], in_=var[:, rows], func=ACT.Abs_reciprocal_sqrt)
-            if first == 2:
-                nc.gpsimd.tensor_tensor(out=shift[:, rows], in0=neg_mean[:, rows], in1=rstd[:, rows], op=ALU.mult)
-
         def statistics(half, l):
             j = ROWS * half + l
             col = slice(j, j + 1)
@@ -414,24 +374,34 @@ def tile_ultralightweightmemory_pa_kernel(
                 scale=float(D),
                 accum_out=sq_sum[:, col],
             )
-            nc.scalar.activation(
-                out=rstd[:, col],
-                in_=sq_sum[:, col],
-                func=ACT.Abs_reciprocal_sqrt,
-                bias=LN_EPS,
-                scale=1.0 / (D * D * D),
+            if half == 0:
+                nc.gpsimd.tensor_scalar(
+                    out=var[:, col],
+                    in0=sq_sum[:, col],
+                    scalar1=1.0 / (D * D * D),
+                    scalar2=LN_EPS,
+                    op0=ALU.mult,
+                    op1=ALU.add,
+                )
+                nc.gpsimd.tensor_tensor(out=rstd[:, col], in0=var[:, col], in1=minus_half[:], op=ALU.pow)
+            else:
+                nc.scalar.activation(
+                    out=rstd[:, col],
+                    in_=sq_sum[:, col],
+                    func=ACT.Abs_reciprocal_sqrt,
+                    bias=LN_EPS,
+                    scale=1.0 / (D * D * D),
+                )
+            nc.gpsimd.tensor_scalar(
+                out=neg_mean[:, col], in0=neg_sum[:, col], scalar1=1.0 / D, scalar2=0.0, op0=ALU.mult, op1=ALU.add
             )
-            nc.scalar.activation(out=neg_mean[:, col], in_=neg_sum[:, col], func=ACT.Copy, scale=1.0 / D)
 
         def normalise(half, l):
             j = ROWS * half + l
             col = slice(j, j + 1)
             ym = y_row(half, l)
             hbm_rows = slice(P * half, P * (half + 1))
-            if (half, l) in ON_SCALAR:
-                nc.scalar.activation(out=ym, in_=ym, func=ACT.Identity, bias=shift[:, col], scale=rstd[:, col])
-                nc.sync.dma_start(out=out_v[hbm_rows, D * l : D * (l + 1)], in_=ym)
-            elif (half, l) in ON_VECTOR:
+            if (half, l) in ON_VECTOR:
                 w = D // LAST_PIECES
                 for z in range(LAST_PIECES):
                     yz = ym[:, w * z : w * (z + 1)]
@@ -453,22 +423,18 @@ def tile_ultralightweightmemory_pa_kernel(
         quantise_waiting(1)
         mean_chunk(1)
         mean_out(0, "s")
+        prepare(ORDER[0], 0)
+        prepare(ORDER[0], 1)
+        quantise_waiting(2)
         mean_chunk(2)
         mean_chunk(3)
         mean_out(1, "v")
         mean_quantise()
         prepare_key(2, 0)
-        prepare_key(2, 1)
-        quantise_waiting(1)
-        prepare(ORDER[0], 0)
-        quantise_waiting(1)
-        prepare(ORDER[0], 1)
-        quantise_waiting(1)
-        prepare_key(3, 0)
-        quantise_waiting(1)
-        prepare_key(3, 1)
+        for ce in range(5, 8):
+            prepare_key(ce // 2, ce % 2)
+            quantise_waiting(1)
         first_matmul(0, 0, range(4))
-        quantise_waiting(1)
         first_matmul(0, 1, range(2))
         quantise_waiting(1)
         first_matmul(0, 1, range(2, 4))
@@ -499,11 +465,9 @@ def tile_ultralightweightmemory_pa_kernel(
                 mean_chunk(6)
             if step >= 2:
                 quantise_waiting(1)
-            if step in (0, 4, 6, 8, 10):
-                first_half_products(ORDER[max(step // 2 - 1, 0)])
+            if step in (0, 3, 5, 7, 9):
+                first_half_products(ORDER[step // 2])
             unit(step)
-        for l in range(ROWS):
-            squares_of(l, 0, 1)
         first_half_products(ORDER[5])
         mean_chunk(7)
         mean_out(3, "s")
@@ -513,8 +477,6 @@ def tile_ultralightweightmemory_pa_kernel(
             prepare(ORDER[6 + h // 2], h % 2)
         quantise_waiting(2)
         first_half_products(ORDER[6])
-        for l in range(2):
-            squares_of(l, 1, 2)
         mean_quantise()
         first_matmul(1, 0, range(4))
         first_matmul(1, 1, range(4))
@@ -526,8 +488,6 @@ def tile_ultralightweightmemory_pa_kernel(
         add(0, 1, 2)
         proj_quantise(0)
         proj_quantise(1)
-        for l in range(2, 4):
-            squares_of(l, 1, 2)
         second_half_z(0)
         second_half_z(1)
         add(0, 0, 3)
@@ -543,17 +503,15 @@ def tile_ultralightweightmemory_pa_kernel(
         second_half_add(0)
         second_half_add(1)
         second_half_z(3)
-        for l in range(2):
-            squares_of(l, 2, 4)
-        first_half_statistics(0)
+        statistics(0, 0)
         normalise(0, 0)
         second_half_gate(2)
-        for l in range(2, 4):
-            squares_of(l, 2, 4)
+        statistics(0, 1)
         second_half_gate(3)
         normalise(0, 1)
-        first_half_statistics(2)
+        statistics(0, 2)
         normalise(0, 2)
+        statistics(0, 3)
         normalise(0, 3)
         second_half_add(2)
         second_half_add(3)

@@ -164,7 +164,7 @@ def tile_ultralightweightmemory_pa_kernel(
                         w0 = e * (D // 2) + 256 * (2 * z + i)
                         nc.tensor.transpose(tp[:, i, u, :], loaded[:, w0 + u : w0 + 256 : 2], ident_f[:])
                 copy_out(
-                    "vs"[z],
+                    "s" if ce in (4, 6) else "vs"[z],
                     group_d_pairs[:, 512 * z : 512 * (z + 1)].rearrange("q (i c u) -> q i c u", i=2, u=2),
                     tp[:].rearrange("q i u c -> q i c u"),
                 )
@@ -392,9 +392,12 @@ def tile_ultralightweightmemory_pa_kernel(
                     bias=LN_EPS,
                     scale=1.0 / (D * D * D),
                 )
-            nc.gpsimd.tensor_scalar(
-                out=neg_mean[:, col], in0=neg_sum[:, col], scalar1=1.0 / D, scalar2=0.0, op0=ALU.mult, op1=ALU.add
-            )
+            if half == 0:
+                nc.gpsimd.tensor_scalar(
+                    out=neg_mean[:, col], in0=neg_sum[:, col], scalar1=1.0 / D, scalar2=0.0, op0=ALU.mult, op1=ALU.add
+                )
+            else:
+                nc.scalar.activation(out=neg_mean[:, col], in_=neg_sum[:, col], func=ACT.Copy, scale=1.0 / D)
 
         def normalise(half, l):
             j = ROWS * half + l
@@ -524,6 +527,7 @@ def tile_ultralightweightmemory_pa_kernel(
         for I in range(2):
             add(1, 1, I)
         multiply(1, 0, 3)
+        nc.scalar.activation(out=table_warm[:], in_=minus_half[:], func=ACT.Abs_reciprocal_sqrt)
         for l in range(2):
             for I in range(2, 4):
                 add(1, l, I)

@@ -425,7 +425,7 @@ def tile_ultralightweightmemory_pa_kernel(
         mean_chunk(0)
         quantise_waiting(1)
         mean_chunk(1)
-        mean_out(0, "s")
+        mean_out(0, "v")
         prepare(ORDER[0], 0)
         prepare(ORDER[0], 1)
         quantise_waiting(2)
@@ -459,7 +459,7 @@ def tile_ultralightweightmemory_pa_kernel(
         for step in range(12):
             if step + 2 < 12:
                 prepare(ORDER[(step + 2) // 2], step % 2)
-            if step == 7:
+            if step == 6:
                 mean_chunk(4)
             if step == 9:
                 mean_chunk(5)
@@ -473,9 +473,9 @@ def tile_ultralightweightmemory_pa_kernel(
             unit(step)
         first_half_products(ORDER[5])
         mean_chunk(7)
-        mean_out(3, "s")
         for step in range(12, 15):
             unit(step)
+        mean_out(3, "v")
         for h in range(4):
             prepare(ORDER[6 + h // 2], h % 2)
         quantise_waiting(2)
@@ -495,11 +495,11 @@ def tile_ultralightweightmemory_pa_kernel(
         second_half_z(1)
         add(0, 0, 3)
         add(0, 1, 3)
+        add(0, 2, 2)
         total(0, 2)
-        for I in range(2, 4):
-            add(0, 2, I)
-            add(0, 3, I)
-        total(2, 2)
+        add(0, 3, 2)
+        add(0, 2, 3)
+        add(0, 3, 3)
         second_half_gate(0)
         second_half_z(2)
         second_half_gate(1)
@@ -512,15 +512,17 @@ def tile_ultralightweightmemory_pa_kernel(
         statistics(0, 1)
         second_half_gate(3)
         normalise(0, 1)
+        second_half_add(2)
+        second_half_add(3)
+        multiply(1, 0, 0)
+        total(2, 2)
         statistics(0, 2)
         normalise(0, 2)
         statistics(0, 3)
         normalise(0, 3)
-        second_half_add(2)
-        second_half_add(3)
-        for I in range(2):
-            multiply(1, 0, I)
-            multiply(1, 1, I)
+        multiply(1, 1, 0)
+        multiply(1, 0, 1)
+        multiply(1, 1, 1)
         for I in range(2):
             add(1, 0, I)
         multiply(1, 0, 2)
@@ -528,19 +530,26 @@ def tile_ultralightweightmemory_pa_kernel(
             add(1, 1, I)
         multiply(1, 0, 3)
         nc.scalar.activation(out=table_warm[:], in_=minus_half[:], func=ACT.Abs_reciprocal_sqrt)
-        for l in range(2):
-            for I in range(2, 4):
-                add(1, l, I)
-            total(ROWS + l, 1)
+        add(1, 0, 2)
+        add(1, 0, 3)
+        add(1, 1, 2)
+        total(4, 1)
+        add(1, 1, 3)
         statistics(1, 0)
         normalise(1, 0)
-        for I in range(2, 4):
-            multiply(1, 1, I)
+        multiply(1, 1, 2)
+        total(5, 1)
+        multiply(1, 1, 3)
         statistics(1, 1)
         normalise(1, 1)
-        add_row(2)
+        for I in range(4):
+            add(1, 2, I)
+        add(1, 3, 0)
+        total(6, 1)
         statistics(1, 2)
-        add_row(3)
+        for I in range(1, 4):
+            add(1, 3, I)
+        total(7, 1)
         normalise(1, 2)
         statistics(1, 3)
         normalise(1, 3)

@@ -30,7 +30,7 @@ SLOT_TILES = (
 )
 ORDER = (("e", 0), ("e", 1), ("a", 0), ("e", 2), ("a", 1), ("e", 3), ("a", 2), ("a", 3))
 ON_VECTOR = ((1, 2), (1, 3))
-MEAN_BANKS = (0, 1, 1, 4)
+MEAN_BANKS = (0, 1, 1, 1)
 PROJ_BANKS = ((2, 3), (0, 1))
 Z_BANKS = (7, 1)
 GATE_BANKS = (4, 5, 6, 0)
@@ -39,7 +39,7 @@ STEP_MEAN = {8: 4, 10: 5, 12: 6, 13: 7}
 MEAN_ENG = "ss"
 STEP_MULT = {3: [(0, 0)], 4: [(1, 0)], 5: [(0, 1)], 6: [(1, 1)], 9: [(0, 2)], 10: [(1, 2)], 13: [(0, 3)], 14: [(1, 3)]}
 STEP_ADD = {7: [(0, 0), (1, 0)], 8: [(2, 0), (3, 0)], 11: [(0, 1), (1, 1)], 12: [(2, 1), (3, 1)], 15: [(0, 2), (1, 2)], 16: [(2, 2), (3, 2)]}
-LOADS = "k0 k1 x0 x1 e0 x2 x3 k2 k3 e1 m0 a0 m1 e2 a1 x4 e3 x5 x6 x7 a2 a3 m2 m3".split()
+LOADS = "k0 k1 x0 x1 e0 x2 x3 k2 k3 e1 m0 a0 m1 e2 a1 x4 e3 x5 x6 a2 x7 a3 m2 m3".split()
 
 
 def tile_ultralightweightmemory_pa_kernel(
@@ -148,7 +148,7 @@ def tile_ultralightweightmemory_pa_kernel(
 
         turn = {"n": 0}
 
-        def transpose_bank(name, banks=3):
+        def transpose_bank(name, banks=4):
             turn["n"] += 1
             return bank(8 - banks + turn["n"] % banks, [P, 2, 2, P], F32, name)
 
@@ -164,7 +164,7 @@ def tile_ultralightweightmemory_pa_kernel(
                         w0 = e * (D // 2) + 256 * (2 * z + i)
                         nc.tensor.transpose(tp[:, i, u, :], loaded[:, w0 + u : w0 + 256 : 2], ident_f[:])
                 copy_out(
-                    "s" if ce in (4, 6) else "vs"[z],
+                    "s" if ce == 4 else "vs"[z],
                     group_d_pairs[:, 512 * z : 512 * (z + 1)].rearrange("q (i c u) -> q i c u", i=2, u=2),
                     tp[:].rearrange("q i u c -> q i c u"),
                 )
@@ -472,13 +472,16 @@ def tile_ultralightweightmemory_pa_kernel(
                 first_half_products(ORDER[step // 2])
             unit(step)
         first_half_products(ORDER[5])
+        prepare(ORDER[6], 0)
         mean_chunk(7)
         for step in range(12, 15):
             unit(step)
+        quantise_waiting(1)
         mean_out(3, "v")
-        for h in range(4):
-            prepare(ORDER[6 + h // 2], h % 2)
-        quantise_waiting(2)
+        prepare(ORDER[6], 1)
+        prepare(ORDER[7], 0)
+        prepare(ORDER[7], 1)
+        quantise_waiting(1)
         first_half_products(ORDER[6])
         mean_quantise()
         first_matmul(1, 0, range(4))

from contextlib import ExitStack

import concourse.masks as masks
import concourse.mybir as mybir

FLOPS = 2 * 128 * 2048 * 1024 * 3

F32 = mybir.dt.float32
BF16 = mybir.dt.bfloat16
U32 = mybir.dt.uint32
U8 = mybir.dt.uint8
FP8X4 = mybir.dt.float8_e4m3fn_x4
ALU = mybir.AluOpType
ACT = mybir.ActivationFunctionType

P = 128
D = 2048
ROWS = 4
CHUNK = 512
LN_EPS = 1e-5
LAST_PIECES = 4

SLOT_TILES = (
    ("k0 k1", "a1 e3", "y10"),
    ("x0 x1", "a2 a3", "y11"),
    ("x2 x3", "y00"),
    ("k2 k3", "y01"),
    ("e0 e1", "x4 x5"),
    ("a0 e2", "x6 x7"),
)
ORDER = (("e", 0), ("e", 1), ("a", 0), ("e", 2), ("a", 1), ("e", 3), ("a", 2), ("a", 3))
ON_VECTOR = ((1, 2), (1, 3))
MEAN_BANKS = (0, 1, 1, 1)
PROJ_BANKS = ((2, 3), (0, 1))
Z_BANKS = (7, 1)
GATE_BANKS = (4, 5, 6, 0)
ADD_BANKS = (2, 3, 7, 1)
STEP_MEAN = {8: 4, 10: 5, 12: 6, 13: 7}
MEAN_ENG = "ss"
STEP_MULT = {3: [(0, 0)], 4: [(1, 0)], 5: [(0, 1)], 6: [(1, 1)], 9: [(0, 2)], 10: [(1, 2)], 13: [(0, 3)], 14: [(1, 3)]}
STEP_ADD = {7: [(0, 0), (1, 0)], 8: [(2, 0), (3, 0)], 11: [(0, 1), (1, 1)], 12: [(2, 1), (3, 1)], 15: [(0, 2), (1, 2)], 16: [(2, 2), (3, 2)]}
LOADS = "k0 k1 x0 x1 e0 x2 x3 k2 k3 e1 m0 a0 m1 e2 a1 x4 e3 x5 x6 a2 x7 a3 m2 m3".split()


def tile_ultralightweightmemory_pa_kernel(
    tc, interface, memory, W_write_key, W_write_erase, W_write_add, out
):
    nc = tc.nc
    slot_of = {}
    for number, tiles in enumerate(SLOT_TILES):
        for names in tiles:
            for part, name in enumerate(names.split()):
                slot_of[name] = (number, part, names)

    with ExitStack() as ctx:
        const = ctx.enter_context(tc.tile_pool(name="const", bufs=1))
        keep = ctx.enter_context(tc.tile_pool(name="keep", bufs=1))
        slots = ctx.enter_context(tc.tile_pool(name="slots", bufs=1))
        grouped = ctx.enter_context(tc.tile_pool(name="grouped", bufs=6))
        psum = ctx.enter_context(tc.psum_pool(name="psum", bufs=1))
        ctx.enter_context(tc.manual_schedule())

        def bank(n, shape, dtype, name):
            return psum.tile(shape, dtype, tag="bank%d" % n, name=name)

        x_v = interface.rearrange("b s d -> (b s) d").rearrange("(T p i) d -> T p (i d)", p=P, i=2)
        wk_v = W_write_key.rearrange("(G p h e) d -> G h p (e d)", p=P, h=2, e=2)
        w2_v = {
            "e": W_write_erase.rearrange("(I h p c) r -> I p h (c r)", h=2, p=P, c=2),
            "a": W_write_add.rearrange("(I h p c) r -> I p h (c r)", h=2, p=P, c=2),
        }
        mem_v = memory.rearrange("b (u l) n -> (b u) (l n)", u=2)
        out_v = out.rearrange("b (u l) n -> (b u) (l n)", u=2)

        mem_sb = [keep.tile([P, ROWS * D], BF16, name="mem%d" % half) for half in range(2)]
        gate_sb = keep.tile([P, D], F32)
        squares = keep.tile([P, D], BF16)
        words = {}
        scales = {}
        for kind in "kea":
            words[kind] = keep.tile([P, 4096], U32, name="words_%s" % kind, align_bytes=64)
            scales[kind] = keep.tile([P, 4096], U8, name="scales_%s" % kind, align_bytes=64)
        mean_bf = keep.tile([P, 2048], BF16, align_bytes=64)
        mean_words = keep.tile([P, 512], U32, align_bytes=64)
        mean_scales = keep.tile([P, 512], U8, align_bytes=64)
        proj_bf = keep.tile([P, 1024], BF16, align_bytes=64)
        proj_words = keep.tile([P, 256], U32, align_bytes=64)
        proj_scales = keep.tile([P, 256], U8, align_bytes=64)
        part_sums = keep.tile([P, 2 * ROWS, 4], F32)
        neg_sum = keep.tile([P, 2 * ROWS], F32)
        neg_mean = keep.tile([P, 2 * ROWS], F32)
        sq_sum = keep.tile([P, 2 * ROWS], F32)
        var = keep.tile([P, ROWS], F32)
        rstd = keep.tile([P, 2 * ROWS], F32)
        table_warm = keep.tile([P, 1], F32)

        raw = {}
        slot_tile = {}

        def slot(name, shape, dtype):
            return slots.tile(shape, dtype, tag="slot%d" % slot_of[name][0], name="slot_%s" % name)

        for load in LOADS:
            kind, idx = load[0], int(load[1])
            if kind == "m":
                half, part = divmod(idx, 2)
                cols = slice(2 * D * part, 2 * D * (part + 1))
                nc.sync.dma_start(out=mem_sb[half][:, cols], in_=mem_v[P * half : P * (half + 1), cols])
                continue
            tile_name = slot_of[load][2]
            if tile_name not in slot_tile:
                slot_tile[tile_name] = slot(load, [P, 8192], BF16)
            t = slot_tile[tile_name][:, 4096 * slot_of[load][1] : 4096 * (slot_of[load][1] + 1)]
            if kind == "k":
                nc.sync.dma_start(out=t, in_=wk_v[idx // 2, idx % 2])
            elif kind == "x":
                nc.sync.dma_start(out=t, in_=x_v[idx])
            else:
                nc.sync.dma_start(out=t.rearrange("p (h x) -> p h x", h=2), in_=w2_v[kind][idx])
            raw[(kind, idx)] = t

        ident_f = const.tile([P, P], F32)
        masks.make_identity(nc, ident_f[:])
        member = const.tile([P, 16], F32)
        nc.vector.tensor_reduce(
            out=member[:], in_=ident_f[:].rearrange("p (n s) -> p n s", s=8), axis=mybir.AxisListType.X, op=ALU.add
        )
        averager = const.tile([P, 16], BF16)
        nc.vector.tensor_scalar_mul(out=averager[:], in0=member[:], scalar1=1.0 / 16.0)
        minus_half = const.tile([P, 1], F32)
        nc.vector.memset(minus_half[:], -0.5)
        nc.scalar.activation(out=table_warm[:], in_=minus_half[:], func=ACT.Sigmoid)

        def copy_out(engine, dst, src):
            if engine == "v":
                nc.vector.tensor_copy(out=dst, in_=src)
            else:
                nc.scalar.copy(out=dst, in_=src)

        def quantise(words_ap, scales_ap, in_ap):
            nc.vector.quantize_mx(out=words_ap.bitcast(FP8X4), scales=scales_ap, in_=in_ap)

        waiting = []

        def quantise_waiting(count):
            for i in range(count):
                waiting.pop(0)()

        turn = {"n": 0}

        def transpose_bank(name, banks=4):
            turn["n"] += 1
            return bank(8 - banks + turn["n"] % banks, [P, 2, 2, P], F32, name)

        def prepare_key(j, e):
            loaded = raw[("k", j)].bitcast(F32)
            ce = 2 * j + e
            group = grouped.tile([P, 2048], BF16, tag="grp", name="gk%d" % ce, align_bytes=64)
            group_d_pairs = group[:].bitcast(F32)
            for z in range(2):
                tp = transpose_bank("tpk%d_%d" % (ce, z), 4)
                for i in range(2):
                    for u in range(2):
                        w0 = e * (D // 2) + 256 * (2 * z + i)
                        nc.tensor.transpose(tp[:, i, u, :], loaded[:, w0 + u : w0 + 256 : 2], ident_f[:])
                copy_out(
                    "s" if ce == 4 else "vs"[z],
                    group_d_pairs[:, 512 * z : 512 * (z + 1)].rearrange("q (i c u) -> q i c u", i=2, u=2),
                    tp[:].rearrange("q i u c -> q i c u"),
                )
            cols = slice(512 * ce, 512 * (ce + 1))
            waiting.append(lambda: quantise(words["k"][:, cols], scales["k"][:, cols], group[:]))

        mean_ps = {}

        def mean_chunk(T):
            if T % 2 == 0:
                mean_ps[T // 2] = bank(MEAN_BANKS[T // 2], [P, 16, 32], F32, "mean%d" % T)
            xt = raw[("x", T)]
            for c in range(16):
                for i in range(2):
                    lo = i * D + 512 * (c // 4)
                    nc.tensor.matmul(
                        mean_ps[T // 2][:, c, 16 * (T % 2) : 16 * (T % 2 + 1)],
                        lhsT=xt[:, lo + c % 4 : lo + 512 : 4],
                        rhs=averager[:],
                        start=(i == 0),
                        stop=(i == 1),
                    )

        def mean_out(pair, engine):
            dst = mean_bf[:].rearrange("p (g h b u t) -> p h u g b t", g=4, h=2, u=2, t=4)
            for u in range(2):
                copy_out(
                    engine,
                    dst[:, pair % 2, u, :, :, :],
                    mean_ps[pair][:].rearrange("p (g t) b -> p g b t", t=4),
                )

        def mean_quantise():
            quantise(mean_words[:, 0:256], mean_scales[:, 0:256], mean_bf[:, 0:1024])
            quantise(mean_words[:, 256:512], mean_scales[:, 256:512], mean_bf[:, 1024:2048])

        proj_ps = {}

        def first_matmul(half, G, ts):
            if ts[0] == 0:
                proj_ps[G] = bank(PROJ_BANKS[half][G], [P, 4, P], F32, "pj%d_%d" % (half, G))
            pj = proj_ps[G]
            for t in ts:
                ce = 4 * G + t
                for g in range(4):
                    lo = 512 * ce + 128 * g
                    nc.tensor.matmul_mx(
                        out=pj[:, t, :],
                        lhsT=words["k"][:, lo : lo + 128].bitcast(FP8X4),
                        lhsT_scale=scales["k"][:, lo : lo + 128],
                        rhs=mean_words[:, 128 * g : 128 * (g + 1)].bitcast(FP8X4),
                        rhs_scale=mean_scales[:, 128 * g : 128 * (g + 1)],
                        start=(g == 0),
                        stop=(g == 3),
                    )

        def proj_out(G, engine):
            copy_out(
                engine,
                proj_bf[:, 512 * G : 512 * (G + 1)].rearrange("p (b t) -> p b t", t=4),
                proj_ps[G][:].rearrange("p t b -> p b t"),
            )

        def proj_quantise(G):
            cols = slice(128 * G, 128 * (G + 1))
            quantise(proj_words[:, cols], proj_scales[:, cols], proj_bf[:, 512 * G : 512 * (G + 1)])

        def prepare(chunk, h):
            kind, I = chunk
            r_pairs = raw[(kind, I)].bitcast(F32)
            group = grouped.tile([P, 2048], BF16, tag="grp", name="g%s%d%d" % (kind, I, h), align_bytes=64)
            group_r_pairs = group[:].bitcast(F32)
            for G in range(2):
                tp = transpose_bank("tp%s%d%d%d" % (kind, I, h, G))
                for c in range(2):
                    for u in range(2):
                        w0 = (h * 2 + c) * 512 + 256 * G
                        nc.tensor.transpose(tp[:, c, u, :], r_pairs[:, w0 + u : w0 + 256 : 2], ident_f[:])
                copy_out(
                    "s",
                    group_r_pairs[:, 512 * G : 512 * (G + 1)].rearrange("q (p c u) -> q p c u", c=2, u=2),
                    tp[:].rearrange("q c u p -> q p c u"),
                )
            cols = slice(512 * (2 * I + h), 512 * (2 * I + h + 1))
            waiting.append(lambda: quantise(words[kind][:, cols], scales[kind][:, cols], group[:]))

        def second_matmul(o_ps, kind, I):
            for h in range(2):
                for G in range(2):
                    lo = 512 * (2 * I + h) + 256 * G
                    nc.tensor.matmul_mx(
                        out=o_ps[:, 256 * h : 256 * (h + 1)],
                        lhsT=proj_words[:, 128 * G : 128 * (G + 1)].bitcast(FP8X4),
                        lhsT_scale=proj_scales[:, 128 * G : 128 * (G + 1)],
                        rhs=words[kind][:, lo : lo + 256].bitcast(FP8X4),
                        rhs_scale=scales[kind][:, lo : lo + 256],
                        start=(G == 0),
                        stop=(G == 1),
                    )

        add_ps = {}
        gate_ps = {}

        def first_half_products(chunk):
            kind, I = chunk
            if kind == "e":
                o_ps = bank(0, [P, CHUNK], F32, "o_e%d" % I)
                second_matmul(o_ps, kind, I)
                nc.scalar.activation(
                    out=gate_sb[:, CHUNK * I : CHUNK * (I + 1)], in_=o_ps[:], func=ACT.Sigmoid, scale=-1.0
                )
            else:
                add_ps[(0, I)] = bank(2 + I % 2, [P, CHUNK], F32, "o_a%d" % I)
                second_matmul(add_ps[(0, I)], kind, I)

        z_ps = {}

        def second_half_z(I):
            z_ps[I] = bank(Z_BANKS[I % 2], [P, 4, P], F32, "zt%d" % I)
            for jj in range(4):
                for G in range(2):
                    lo = 512 * (2 * I + jj // 2) + 256 * G + 128 * (jj % 2)
                    nc.tensor.matmul_mx(
                        out=z_ps[I][:, jj, :],
                        lhsT=words["e"][:, lo : lo + 128].bitcast(FP8X4),
                        lhsT_scale=scales["e"][:, lo : lo + 128],
                        rhs=proj_words[:, 128 * G : 128 * (G + 1)].bitcast(FP8X4),
                        rhs_scale=proj_scales[:, 128 * G : 128 * (G + 1)],
                        start=(G == 0),
                        stop=(G == 1),
                    )

        def second_half_gate(I):
            nc.scalar.activation(
                out=gate_sb[:, CHUNK * I : CHUNK * (I + 1)],
                in_=z_ps[I][:].rearrange("p j b -> p (j b)"),
                func=ACT.Sigmoid,
                scale=-1.0,
            )
            gate_ps[I] = bank(GATE_BANKS[I], [P, CHUNK], F32, "gps%d" % I)
            for jj in range(4):
                lo = CHUNK * I + 128 * jj
                nc.tensor.transpose(gate_ps[I][:, 128 * jj : 128 * (jj + 1)], gate_sb[:, lo : lo + 128], ident_f[:])

        def second_half_add(I):
            add_ps[(1, I)] = bank(ADD_BANKS[I], [P, CHUNK], F32, "a1_%d" % I)
            second_matmul(add_ps[(1, I)], "a", I)

        y_tile = {}

        def y_row(half, l):
            return y_tile[(half, l // 2)][:, D * (l % 2) : D * (l % 2 + 1)]

        def multiply(half, k, I):
            if (half, k) not in y_tile:
                y_tile[(half, k)] = slot("y%d%d" % (half, k), [P, 2 * D], F32)
            ns = slice(CHUNK * I, CHUNK * (I + 1))
            yv = y_tile[(half, k)][:].rearrange("p (l n) -> p l n", l=2)
            mv = mem_sb[half][:].rearrange("p (l n) -> p l n", l=ROWS)
            nc.vector.tensor_tensor(
                out=yv[:, :, ns],
                in0=mv[:, 2 * k : 2 * k + 2, ns],
                in1=(gate_sb[:, ns] if half == 0 else gate_ps[I][:]).unsqueeze(1).to_broadcast([P, 2, CHUNK]),
                op=ALU.mult,
            )

        def add(half, l, I):
            ym = y_row(half, l)[:, CHUNK * I : CHUNK * (I + 1)]
            nc.vector.scalar_tensor_tensor(
                out=ym,
                in0=ym,
                scalar=1.0,
                in1=add_ps[(half, I)][:],
                op0=ALU.mult,
                op1=ALU.add,
                accum_out=part_sums[:, ROWS * half + l, I : I + 1],
            )

        def total(first, count):
            nc.vector.tensor_reduce(
                out=neg_sum[:, first : first + count],
                in_=part_sums[:, first : first + count, :],
                axis=mybir.AxisListType.X,
                op=ALU.add,
                negate=True,
            )

        def add_chunk(I):
            for l in range(ROWS):
                add(0, l, I)
            if I == 3:
                total(0, ROWS)

        def add_row(l):
            for I in range(4):
                add(1, l, I)
            total(ROWS + l, 1)

        def statistics(half, l):
            j = ROWS * half + l
            col = slice(j, j + 1)
            nc.scalar.activation(
                out=squares[:],
                in_=y_row(half, l),
                func=ACT.Square,
                bias=neg_sum[:, col],
                scale=float(D),
                accum_out=sq_sum[:, col],
            )
            if half == 0:
                nc.gpsimd.tensor_scalar(
                    out=var[:, col],
                    in0=sq_sum[:, col],
                    scalar1=1.0 / (D * D * D),
                    scalar2=LN_EPS,
                    op0=ALU.mult,
                    op1=ALU.add,
                )
                nc.gpsimd.tensor_tensor(out=rstd[:, col], in0=var[:, col], in1=minus_half[:], op=ALU.pow)
            else:
                nc.scalar.activation(
                    out=rstd[:, col],
                    in_=sq_sum[:, col],
                    func=ACT.Abs_reciprocal_sqrt,
                    bias=LN_EPS,
                    scale=1.0 / (D * D * D),
                )
            if half == 0:
                nc.gpsimd.tensor_scalar(
                    out=neg_mean[:, col], in0=neg_sum[:, col], scalar1=1.0 / D, scalar2=0.0, op0=ALU.mult, op1=ALU.add
                )
            else:
                nc.scalar.activation(out=neg_mean[:, col], in_=neg_sum[:, col], func=ACT.Copy, scale=1.0 / D)

        def normalise(half, l):
            j = ROWS * half + l
            col = slice(j, j + 1)
            ym = y_row(half, l)
            hbm_rows = slice(P * half, P * (half + 1))
            if (half, l) in ON_VECTOR:
                w = D // LAST_PIECES
                for z in range(LAST_PIECES):
                    yz = ym[:, w * z : w * (z + 1)]
                    nc.vector.tensor_scalar(
                        out=yz, in0=yz, scalar1=neg_mean[:, col], scalar2=rstd[:, col], op0=ALU.add, op1=ALU.mult
                    )
                    nc.sync.dma_start(out=out_v[hbm_rows, D * l + w * z : D * l + w * (z + 1)], in_=yz)
            else:
                nc.gpsimd.tensor_scalar(
                    out=ym, in0=ym, scalar1=neg_mean[:, col], scalar2=rstd[:, col], op0=ALU.add, op1=ALU.mult
                )
                nc.sync.dma_start(out=out_v[hbm_rows, D * l : D * (l + 1)], in_=ym)

        for ce in range(4):
            prepare_key(ce // 2, ce % 2)
            if ce > 0:
                quantise_waiting(1)
        mean_chunk(0)
        quantise_waiting(1)
        mean_chunk(1)
        mean_out(0, "v")
        prepare(ORDER[0], 0)
        prepare(ORDER[0], 1)
        quantise_waiting(2)
        mean_chunk(2)
        mean_chunk(3)
        mean_out(1, "v")
        mean_quantise()
        prepare_key(2, 0)
        for ce in range(5, 8):
            prepare_key(ce // 2, ce % 2)
            quantise_waiting(1)
        first_matmul(0, 0, range(4))
        first_matmul(0, 1, range(2))
        quantise_waiting(1)
        first_matmul(0, 1, range(2, 4))
        proj_out(0, "s")
        proj_out(1, "v")
        proj_quantise(0)
        proj_quantise(1)
        def unit(step):
            j, part = divmod(step - 2 if step < 4 else step - 3, 2)
            if step < 2 or step == 4:
                return
            kind, I = ORDER[j]
            if kind == "e":
                multiply(0, part, I)
            else:
                add(0, 2 * part, I)
                add(0, 2 * part + 1, I)

        for step in range(12):
            if step + 2 < 12:
                prepare(ORDER[(step + 2) // 2], step % 2)
            if step == 6:
                mean_chunk(4)
            if step == 9:
                mean_chunk(5)
                mean_out(2, "s")
            if step == 11:
                mean_chunk(6)
            if step >= 2:
                quantise_waiting(1)
            if step in (0, 3, 5, 7, 9):
                first_half_products(ORDER[step // 2])
            unit(step)
        first_half_products(ORDER[5])
        prepare(ORDER[6], 0)
        mean_chunk(7)
        for step in range(12, 15):
            unit(step)
        quantise_waiting(1)
        mean_out(3, "v")
        prepare(ORDER[6], 1)
        prepare(ORDER[7], 0)
        prepare(ORDER[7], 1)
        quantise_waiting(1)
        first_half_products(ORDER[6])
        mean_quantise()
        first_matmul(1, 0, range(4))
        first_matmul(1, 1, range(4))
        proj_out(0, "s")
        proj_out(1, "s")
        quantise_waiting(2)
        first_half_products(ORDER[7])
        add(0, 0, 2)
        add(0, 1, 2)
        proj_quantise(0)
        proj_quantise(1)
        second_half_z(0)
        second_half_z(1)
        add(0, 0, 3)
        add(0, 1, 3)
        add(0, 2, 2)
        total(0, 2)
        add(0, 3, 2)
        add(0, 2, 3)
        add(0, 3, 3)
        second_half_gate(0)
        second_half_z(2)
        second_half_gate(1)
        second_half_add(0)
        second_half_add(1)
        second_half_z(3)
        statistics(0, 0)
        normalise(0, 0)
        second_half_gate(2)
        statistics(0, 1)
        second_half_gate(3)
        normalise(0, 1)
        second_half_add(2)
        second_half_add(3)
        multiply(1, 0, 0)
        total(2, 2)
        statistics(0, 2)
        normalise(0, 2)
        statistics(0, 3)
        normalise(0, 3)
        multiply(1, 1, 0)
        multiply(1, 0, 1)
        multiply(1, 1, 1)
        for I in range(2):
            add(1, 0, I)
        multiply(1, 0, 2)
        for I in range(2):
            add(1, 1, I)
        multiply(1, 0, 3)
        nc.scalar.activation(out=table_warm[:], in_=minus_half[:], func=ACT.Abs_reciprocal_sqrt)
        add(1, 0, 2)
        add(1, 0, 3)
        add(1, 1, 2)
        total(4, 1)
        add(1, 1, 3)
        statistics(1, 0)
        normalise(1, 0)
        multiply(1, 1, 2)
        total(5, 1)
        multiply(1, 1, 3)
        statistics(1, 1)
        normalise(1, 1)
        for I in range(4):
            add(1, 2, I)
        add(1, 3, 0)
        total(6, 1)
        statistics(1, 2)
        for I in range(1, 4):
            add(1, 3, I)
        total(7, 1)
        normalise(1, 2)
        statistics(1, 3)
        normalise(1, 3)
